import numpy as np
import ml_dtypes


def mxq(x, axis, fmt="e4m3"):
    dtype, down = {"e4m3": (ml_dtypes.float8_e4m3fn, 7), "e5m2": (ml_dtypes.float8_e5m2, 14)}[fmt]
    v = np.moveaxis(np.asarray(x, np.float32).astype(ml_dtypes.bfloat16).astype(np.float64), axis, -1)
    blocks = v.reshape(v.shape[:-1] + (-1, 32))
    amax = np.abs(blocks).max(-1, keepdims=True)
    byte = np.maximum(np.where(amax > 0, np.frexp(amax)[1] - 1 + 127, 0) - down, 1)
    scale = np.exp2(byte - 127.0)
    codes = (blocks / scale).astype(np.float32).astype(dtype).astype(np.float64)
    return np.moveaxis((codes * scale).reshape(v.shape), -1, axis)


WIDE = False


def mx_kscale(k):
    if not WIDE:
        return np.ones(k)
    levels = np.array([10, -10, 5, -5, 0])
    a = np.random.permutation(np.resize(levels, k // 512 * 4)).reshape(k // 512, 4)
    idx = np.arange(k)
    return np.exp2(a[idx // 512, idx % 128 // 32])


BF16 = ml_dtypes.bfloat16


def bf(x):
    return np.asarray(x, np.float32).astype(BF16)


def f64(x):
    return np.asarray(x).astype(np.float64)


N, D, DO, R0, R1, R2, R3, R4 = 2560, 512, 512, 1, 2, 4, 10, 25
SCALES = (R0, R1, R2, R3)
NS = len(SCALES)


def setup_inputs():
    s = mx_kscale(D)
    return {"inputs_c_e": bf(np.random.standard_normal((N, D)) * s),
            "Ws": bf(np.random.standard_normal((NS, DO, D)) / np.sqrt(D) / s),
            "bs": bf(np.random.standard_normal((NS, DO)) * 0.5)}


def reference(inputs_c_e, Ws, bs):
    x, W, b = f64(inputs_c_e), f64(Ws), f64(bs)
    outs = []
    for i, r in enumerate(SCALES):
        groups = N // r
        sums = x.reshape(groups, r, D).sum(axis=1)
        h = np.maximum((mxq(sums, 1, "e4m3") @ mxq(W[i].T, 0, "e4m3")) + b[i], 0.0) / r
        outs.append(np.repeat(h, r, axis=0))
    return np.concatenate(outs, axis=0)

@@ -1,0 +1,257 @@
+from contextlib import ExitStack
+
+import concourse.mybir as mybir
+from concourse.masks import make_identity
+
+F32 = mybir.dt.float32
+BF16 = mybir.dt.bfloat16
+U32 = mybir.dt.uint32
+U8 = mybir.dt.uint8
+FP8X4 = mybir.dt.float8_e4m3fn_x4
+ALU = mybir.AluOpType
+ACT = mybir.ActivationFunctionType
+
+P = 128
+N = 2560
+D = 512
+DO = 512
+T = N // P
+CH = 4
+NCH = T // CH
+SCALES = (1, 2, 4, 10)
+FLOPS = 2 * sum(N // r for r in SCALES) * D * DO
+
+E2_ORDER = ("g", "s")
+CAST2 = "g"
+CAST4 = "s"
+
+
+def tile_contractexpand_pa_kernel(tc, inputs_c_e, Ws, bs, out):
+    nc = tc.nc
+    x_rows = inputs_c_e.rearrange("(p t) k -> p (t k)", t=T)
+    w_rows = Ws.rearrange("i (p c) k -> i p (c k)", c=4)
+    b_row = bs.rearrange("(o i) d -> o (i d)", o=1)
+    out_rows = out.rearrange("(i p t) d -> i p t d", i=4, t=T)
+
+    with ExitStack() as ctx:
+        const = ctx.enter_context(tc.tile_pool(name="const", bufs=1))
+        keep = ctx.enter_context(tc.tile_pool(name="keep", bufs=1))
+        sums = ctx.enter_context(tc.tile_pool(name="sums", bufs=3))
+        wstage = ctx.enter_context(tc.tile_pool(name="wstage", bufs=2))
+        tmpp = ctx.enter_context(tc.tile_pool(name="tmpp", bufs=3))
+        outp = ctx.enter_context(tc.tile_pool(name="outp", bufs=8))
+        pst = ctx.enter_context(tc.psum_pool(name="pst", bufs=3))
+        psy = ctx.enter_context(tc.psum_pool(name="psy", bufs=5))
+
+        ident = const.tile([P, P], F32, name="ident")
+        make_identity(nc, ident[:])
+        ones = const.tile([P, P], BF16, name="ones")
+        nc.vector.memset(ones[:], 1.0)
+        bz = const.tile([P, 4 * DO], BF16, name="bz")
+        nc.vector.memset(bz[:], 0.0)
+        nc.scalar.dma_start(out=bz[0:1, :], in_=b_row)
+        bias = const.tile([P, 4, DO], F32, name="bias")
+
+        x_sb = [keep.tile([P, CH * D], BF16, name="x_sb%d" % j) for j in range(NCH)]
+        w_sb = [keep.tile([P, 4 * D], BF16, name="w_sb%d" % i) for i in range(4)]
+
+        def load_x(j):
+            nc.sync.dma_start(out=x_sb[j][:], in_=x_rows[:, j * CH * D : (j + 1) * CH * D])
+
+        def load_w(i):
+            nc.sync.dma_start(out=w_sb[i][:], in_=w_rows[i])
+
+        load_x(0)
+        load_w(2)
+        load_w(1)
+        load_w(0)
+        load_x(1)
+        load_x(2)
+        load_w(3)
+        load_x(3)
+        load_x(4)
+
+        for i in range(4):
+            pb = psy.tile([P, DO], F32, name="pb", tag="y")
+            nc.tensor.matmul(out=pb[:], lhsT=ones[:], rhs=bz[:, i * DO : (i + 1) * DO], start=True, stop=True)
+            nc.scalar.copy(out=bias[:, i, :], in_=pb[:])
+
+        xg = [keep.tile([P, CH * D], BF16, name="xg%d" % j, align_bytes=64) for j in range(NCH)]
+        xc = [keep.tile([P, CH * P], U32, name="xc%d" % j, align_bytes=64) for j in range(NCH)]
+        xs = [keep.tile([P, CH * P], U8, name="xs%d" % j, align_bytes=64) for j in range(NCH)]
+        wc = [keep.tile([P, DO], U32, name="wc%d" % i, align_bytes=64) for i in range(4)]
+        ws = [keep.tile([P, DO], U8, name="ws%d" % i, align_bytes=64) for i in range(4)]
+
+        def prep_w(i):
+            w32 = w_sb[i][:].bitcast(F32)
+            wg = wstage.tile([P, 4 * DO], BF16, name="wg", tag="wg", align_bytes=64)
+            wg32 = wg[:].bitcast(F32).rearrange("q (p h m) -> q p h m", h=2, m=4)
+            for h in range(2):
+                pt = pst.tile([P, 512], F32, name="pt", tag="pt")
+                for m in range(4):
+                    nc.tensor.transpose(
+                        pt[:, m * P : (m + 1) * P], w32[:, (4 * h + m) * P : (4 * h + m + 1) * P], ident[:]
+                    )
+                nc.scalar.copy(out=wg32[:, :, h, :], in_=pt[:].rearrange("q (m p) -> q p m", m=4))
+            nc.vector.quantize_mx(out=wc[i][:].bitcast(FP8X4), scales=ws[i][:], in_=wg[:])
+
+        def tr_x(j):
+            x32 = x_sb[j][:].bitcast(F32)
+            xg32 = xg[j][:].bitcast(F32).rearrange("q (t p u) -> q t p u", t=CH, u=2)
+            for h in range(2):
+                pt = pst.tile([P, 512], F32, name="pt", tag="pt")
+                for m in range(4):
+                    nc.tensor.transpose(
+                        pt[:, m * P : (m + 1) * P], x32[:, (4 * h + m) * P : (4 * h + m + 1) * P], ident[:]
+                    )
+                nc.scalar.copy(
+                    out=xg32[:, 2 * h : 2 * h + 2, :, :],
+                    in_=pt[:].rearrange("q (t u p) -> q t p u", t=2, u=2),
+                )
+
+        def cast(eng, dst, src):
+            if eng == "g":
+                nc.gpsimd.tensor_scalar(out=dst, in0=src, scalar1=1.0, scalar2=0.0, op0=ALU.mult, op1=ALU.add)
+            elif eng == "s":
+                nc.scalar.copy(out=dst, in_=src)
+            else:
+                nc.vector.tensor_copy(out=dst, in_=src)
+
+        s2f = {}
+        s4f = {}
+        acc = {}
+        s2b = {}
+        s4b = {}
+        s10b = {}
+
+        def do_sums(j):
+            xg4 = xg[j][:].rearrange("q (g j n) -> q g j n", g=2, j=2)
+            a = sums.tile([P, 2, D], F32, name="s2f", tag="s2f")
+            s2f[j] = a
+            nc.vector.tensor_tensor(out=a[:], in0=xg4[:, :, 0, :], in1=xg4[:, :, 1, :], op=ALU.add)
+            b = sums.tile([P, D], F32, name="s4f", tag="s4f")
+            s4f[j] = b
+            nc.vector.tensor_tensor(out=b[:], in0=a[:, 0, :], in1=a[:, 1, :], op=ALU.add)
+            a16 = sums.tile([P, 2 * D], BF16, name="s2b", tag="s2b", align_bytes=64)
+            s2b[j] = a16
+            cast(CAST2, a16[:], a[:].rearrange("q g n -> q (g n)"))
+            b16 = sums.tile([P, D], BF16, name="s4b", tag="s4b", align_bytes=64)
+            s4b[j] = b16
+            cast(CAST4, b16[:], b[:])
+            if j == 1:
+                c = sums.tile([P, D], F32, name="acc", tag="acc")
+                acc[0] = c
+                nc.vector.tensor_tensor(out=c[:], in0=s4f[0][:], in1=s4f[1][:], op=ALU.add)
+            if j == 2:
+                c16 = sums.tile([P, D], BF16, name="s10b", tag="s10b", align_bytes=64)
+                s10b[0] = c16
+                nc.vector.tensor_tensor(out=c16[:], in0=acc[0][:], in1=a[:, 0, :], op=ALU.add)
+            if j == 3:
+                c = sums.tile([P, D], F32, name="acc", tag="acc")
+                acc[1] = c
+                nc.vector.tensor_tensor(out=c[:], in0=s2f[2][:, 1, :], in1=b[:], op=ALU.add)
+            if j == 4:
+                c16 = sums.tile([P, D], BF16, name="s10b", tag="s10b", align_bytes=64)
+                s10b[1] = c16
+                nc.vector.tensor_tensor(out=c16[:], in0=acc[1][:], in1=b[:], op=ALU.add)
+
+        s2c = {}
+        s4c = {}
+        s10c = {}
+
+        def quant(src, width, tagname):
+            c = sums.tile([P, width // 4], U32, name=tagname + "c", tag=tagname + "c", align_bytes=64)
+            s = sums.tile([P, width // 4], U8, name=tagname + "s", tag=tagname + "s", align_bytes=64)
+            nc.vector.quantize_mx(out=c[:].bitcast(FP8X4), scales=s[:], in_=src)
+            return (c, s)
+
+        def do_quant(j):
+            nc.vector.quantize_mx(out=xc[j][:].bitcast(FP8X4), scales=xs[j][:], in_=xg[j][:])
+            s4c[j] = quant(s4b[j][:], D, "q4")
+            s2c[j] = quant(s2b[j][:], 2 * D, "q2")
+            if j == 2:
+                s10c[0] = quant(s10b[0][:], D, "q10")
+            if j == 4:
+                s10c[1] = quant(s10b[1][:], D, "q10")
+
+        def mx_bias(codes, scales, col, i, dst):
+            y = psy.tile([P, DO], F32, name="y", tag="y")
+            nc.tensor.matmul_mx(
+                out=y[:],
+                lhsT=codes[:, col * P : (col + 1) * P].bitcast(FP8X4),
+                lhsT_scale=scales[:, col * P : (col + 1) * P],
+                rhs=wc[i][:].bitcast(FP8X4),
+                rhs_scale=ws[i][:],
+                start=True,
+                stop=True,
+            )
+            nc.vector.tensor_tensor(out=dst, in0=y[:], in1=bias[:, i, :], op=ALU.add)
+
+        counter = [0]
+
+        def relu_scale(dst, src, r):
+            eng = E2_ORDER[counter[0] % len(E2_ORDER)]
+            counter[0] += 1
+            if eng == "s":
+                nc.scalar.activation(out=dst, in_=src, func=ACT.Relu, scale=1.0 / r)
+            elif eng == "g":
+                nc.gpsimd.tensor_scalar(out=dst, in0=src, scalar1=0.0, scalar2=1.0 / r, op0=ALU.max, op1=ALU.mult)
+            else:
+                nc.vector.tensor_scalar(out=dst, in0=src, scalar1=0.0, scalar2=1.0 / r, op0=ALU.max, op1=ALU.mult)
+
+        def unit_r4(j):
+            tmp = tmpp.tile([P, 2, DO], F32, name="tmp", tag="tmp")
+            mx_bias(s4c[j][0], s4c[j][1], 0, 2, tmp[:, 0, :])
+            ob = outp.tile([P, CH, DO], F32, name="ob", tag="ob")
+            relu_scale(ob[:], tmp[:, 0:1, :].to_broadcast([P, CH, DO]), 4)
+            nc.sync.dma_start(out=out_rows[2, :, j * CH : (j + 1) * CH, :], in_=ob[:])
+
+        def unit_r2(j):
+            tmp = tmpp.tile([P, 2, DO], F32, name="tmp", tag="tmp")
+            for g in range(2):
+                mx_bias(s2c[j][0], s2c[j][1], g, 1, tmp[:, g, :])
+            ob = outp.tile([P, CH, DO], F32, name="ob", tag="ob")
+            relu_scale(
+                ob[:].rearrange("p (g j) d -> p g j d", j=2),
+                tmp[:].unsqueeze(2).to_broadcast([P, 2, 2, DO]),
+                2,
+            )
+            nc.sync.dma_start(out=out_rows[1, :, j * CH : (j + 1) * CH, :], in_=ob[:])
+
+        def unit_r1(j):
+            ob = outp.tile([P, CH, DO], F32, name="ob", tag="ob")
+            for t in range(CH):
+                mx_bias(xc[j], xs[j], t, 0, ob[:, t, :])
+            relu_scale(ob[:], ob[:], 1)
+            nc.sync.dma_start(out=out_rows[0, :, j * CH : (j + 1) * CH, :], in_=ob[:])
+
+        def unit_r10(g):
+            tmp = tmpp.tile([P, 2, DO], F32, name="tmp", tag="tmp")
+            mx_bias(s10c[g][0], s10c[g][1], 0, 3, tmp[:, 0, :])
+            row = 10 * g
+            for n in (4, 4, 2):
+                ob = outp.tile([P, CH, DO], F32, name="ob", tag="ob")
+                relu_scale(ob[:, 0:n, :], tmp[:, 0:1, :].to_broadcast([P, n, DO]), 10)
+                nc.sync.dma_start(out=out_rows[3, :, row : row + n, :], in_=ob[:, 0:n, :])
+                row += n
+
+        tr_x(0)
+        prep_w(2)
+        do_sums(0)
+        prep_w(1)
+        prep_w(0)
+        do_quant(0)
+        for j in range(NCH):
+            if j + 1 < NCH:
+                tr_x(j + 1)
+                if j == 0:
+                    prep_w(3)
+                do_sums(j + 1)
+                do_quant(j + 1)
+            unit_r4(j)
+            if j == 2:
+                unit_r10(0)
+            if j == 4:
+                unit_r10(1)
+            unit_r2(j)
+            unit_r1(j)

@@ -21,9 +21,8 @@ NCH = T // CH
 SCALES = (1, 2, 4, 10)
 FLOPS = 2 * sum(N // r for r in SCALES) * D * DO
 
-E2_ORDER = ("g", "s")
 CAST2 = "g"
-CAST4 = "s"
+CAST4 = "g"
 
 
 def tile_contractexpand_pa_kernel(tc, inputs_c_e, Ws, bs, out):
@@ -38,18 +37,17 @@ def tile_contractexpand_pa_kernel(tc, inputs_c_e, Ws, bs, out):
         keep = ctx.enter_context(tc.tile_pool(name="keep", bufs=1))
         sums = ctx.enter_context(tc.tile_pool(name="sums", bufs=3))
         wstage = ctx.enter_context(tc.tile_pool(name="wstage", bufs=2))
-        tmpp = ctx.enter_context(tc.tile_pool(name="tmpp", bufs=3))
-        outp = ctx.enter_context(tc.tile_pool(name="outp", bufs=8))
+        outp = ctx.enter_context(tc.tile_pool(name="outp", bufs=7))
+        outp10 = ctx.enter_context(tc.tile_pool(name="outp10", bufs=2))
         pst = ctx.enter_context(tc.psum_pool(name="pst", bufs=3))
         psy = ctx.enter_context(tc.psum_pool(name="psy", bufs=5))
 
+        bz = const.tile([P, 4 * DO], BF16, name="bz")
+        nc.vector.memset(bz[:], 0.0)
         ident = const.tile([P, P], F32, name="ident")
         make_identity(nc, ident[:])
         ones = const.tile([P, P], BF16, name="ones")
         nc.vector.memset(ones[:], 1.0)
-        bz = const.tile([P, 4 * DO], BF16, name="bz")
-        nc.vector.memset(bz[:], 0.0)
-        nc.scalar.dma_start(out=bz[0:1, :], in_=b_row)
         bias = const.tile([P, 4, DO], F32, name="bias")
 
         x_sb = [keep.tile([P, CH * D], BF16, name="x_sb%d" % j) for j in range(NCH)]
@@ -63,6 +61,7 @@ def tile_contractexpand_pa_kernel(tc, inputs_c_e, Ws, bs, out):
 
         load_x(0)
         load_w(2)
+        nc.sync.dma_start(out=bz[0:1, :], in_=b_row)
         load_w(1)
         load_w(0)
         load_x(1)
@@ -71,10 +70,11 @@ def tile_contractexpand_pa_kernel(tc, inputs_c_e, Ws, bs, out):
         load_x(3)
         load_x(4)
 
-        for i in range(4):
-            pb = psy.tile([P, DO], F32, name="pb", tag="y")
-            nc.tensor.matmul(out=pb[:], lhsT=ones[:], rhs=bz[:, i * DO : (i + 1) * DO], start=True, stop=True)
-            nc.scalar.copy(out=bias[:, i, :], in_=pb[:])
+        def prep_bias():
+            for i in range(4):
+                pb = psy.tile([P, DO], F32, name="pb", tag="y")
+                nc.tensor.matmul(out=pb[:], lhsT=ones[:], rhs=bz[:, i * DO : (i + 1) * DO], start=True, stop=True)
+                nc.scalar.copy(out=bias[:, i, :], in_=pb[:])
 
         xg = [keep.tile([P, CH * D], BF16, name="xg%d" % j, align_bytes=64) for j in range(NCH)]
         xc = [keep.tile([P, CH * P], U32, name="xc%d" % j, align_bytes=64) for j in range(NCH)]
@@ -187,57 +187,48 @@ def tile_contractexpand_pa_kernel(tc, inputs_c_e, Ws, bs, out):
             )
             nc.vector.tensor_tensor(out=dst, in0=y[:], in1=bias[:, i, :], op=ALU.add)
 
-        counter = [0]
+        def relu_scale(rows, r):
+            nc.scalar.activation(out=rows, in_=rows, func=ACT.Relu, scale=1.0 / r)
 
-        def relu_scale(dst, src, r):
-            eng = E2_ORDER[counter[0] % len(E2_ORDER)]
-            counter[0] += 1
-            if eng == "s":
-                nc.scalar.activation(out=dst, in_=src, func=ACT.Relu, scale=1.0 / r)
-            elif eng == "g":
-                nc.gpsimd.tensor_scalar(out=dst, in0=src, scalar1=0.0, scalar2=1.0 / r, op0=ALU.max, op1=ALU.mult)
-            else:
-                nc.vector.tensor_scalar(out=dst, in0=src, scalar1=0.0, scalar2=1.0 / r, op0=ALU.max, op1=ALU.mult)
+        def repeat(dst, src):
+            nc.gpsimd.tensor_scalar(out=dst, in0=src, scalar1=1.0, scalar2=0.0, op0=ALU.mult, op1=ALU.add)
 
         def unit_r4(j):
-            tmp = tmpp.tile([P, 2, DO], F32, name="tmp", tag="tmp")
-            mx_bias(s4c[j][0], s4c[j][1], 0, 2, tmp[:, 0, :])
             ob = outp.tile([P, CH, DO], F32, name="ob", tag="ob")
-            relu_scale(ob[:], tmp[:, 0:1, :].to_broadcast([P, CH, DO]), 4)
+            mx_bias(s4c[j][0], s4c[j][1], 0, 2, ob[:, 0, :])
+            relu_scale(ob[:, 0, :], 4)
+            repeat(ob[:, 1:CH, :], ob[:, 0:1, :].to_broadcast([P, CH - 1, DO]))
             nc.sync.dma_start(out=out_rows[2, :, j * CH : (j + 1) * CH, :], in_=ob[:])
 
         def unit_r2(j):
-            tmp = tmpp.tile([P, 2, DO], F32, name="tmp", tag="tmp")
-            for g in range(2):
-                mx_bias(s2c[j][0], s2c[j][1], g, 1, tmp[:, g, :])
             ob = outp.tile([P, CH, DO], F32, name="ob", tag="ob")
-            relu_scale(
-                ob[:].rearrange("p (g j) d -> p g j d", j=2),
-                tmp[:].unsqueeze(2).to_broadcast([P, 2, 2, DO]),
-                2,
-            )
+            ob4 = ob[:].rearrange("p (g j) d -> p g j d", j=2)
+            for g in range(2):
+                mx_bias(s2c[j][0], s2c[j][1], g, 1, ob4[:, g, 0, :])
+            relu_scale(ob4[:, :, 0, :], 2)
+            repeat(ob4[:, :, 1, :], ob4[:, :, 0, :])
             nc.sync.dma_start(out=out_rows[1, :, j * CH : (j + 1) * CH, :], in_=ob[:])
 
         def unit_r1(j):
             ob = outp.tile([P, CH, DO], F32, name="ob", tag="ob")
             for t in range(CH):
                 mx_bias(xc[j], xs[j], t, 0, ob[:, t, :])
-            relu_scale(ob[:], ob[:], 1)
+            relu_scale(ob[:], 1)
             nc.sync.dma_start(out=out_rows[0, :, j * CH : (j + 1) * CH, :], in_=ob[:])
 
         def unit_r10(g):
-            tmp = tmpp.tile([P, 2, DO], F32, name="tmp", tag="tmp")
-            mx_bias(s10c[g][0], s10c[g][1], 0, 3, tmp[:, 0, :])
-            row = 10 * g
-            for n in (4, 4, 2):
-                ob = outp.tile([P, CH, DO], F32, name="ob", tag="ob")
-                relu_scale(ob[:, 0:n, :], tmp[:, 0:1, :].to_broadcast([P, n, DO]), 10)
-                nc.sync.dma_start(out=out_rows[3, :, row : row + n, :], in_=ob[:, 0:n, :])
-                row += n
+            ob10 = outp10.tile([P, 5, DO], F32, name="ob10", tag="ob10")
+            mx_bias(s10c[g][0], s10c[g][1], 0, 3, ob10[:, 0, :])
+            relu_scale(ob10[:, 0, :], 10)
+            repeat(ob10[:, 1:5, :], ob10[:, 0:1, :].to_broadcast([P, 4, DO]))
+            for h in range(2):
+                row = 10 * g + 5 * h
+                nc.sync.dma_start(out=out_rows[3, :, row : row + 5, :], in_=ob10[:])
 
         tr_x(0)
         prep_w(2)
         do_sums(0)
+        prep_bias()
         prep_w(1)
         prep_w(0)
         do_quant(0)

@@ -23,6 +23,9 @@ FLOPS = 2 * sum(N // r for r in SCALES) * D * DO
 
 CAST2 = "g"
 CAST4 = "g"
+EXP4 = (False, False, False, False, False)
+EXP10 = (False, False)
+EXP2 = False
 
 
 def tile_contractexpand_pa_kernel(tc, inputs_c_e, Ws, bs, out):
@@ -62,19 +65,18 @@ def tile_contractexpand_pa_kernel(tc, inputs_c_e, Ws, bs, out):
         load_x(0)
         load_w(2)
         nc.sync.dma_start(out=bz[0:1, :], in_=b_row)
-        load_w(1)
-        load_w(0)
         load_x(1)
         load_x(2)
         load_w(3)
         load_x(3)
         load_x(4)
+        load_w(1)
+        load_w(0)
 
-        def prep_bias():
-            for i in range(4):
-                pb = psy.tile([P, DO], F32, name="pb", tag="y")
-                nc.tensor.matmul(out=pb[:], lhsT=ones[:], rhs=bz[:, i * DO : (i + 1) * DO], start=True, stop=True)
-                nc.scalar.copy(out=bias[:, i, :], in_=pb[:])
+        def prep_bias(i):
+            pb = psy.tile([P, DO], F32, name="pb", tag="y")
+            nc.tensor.matmul(out=pb[:], lhsT=ones[:], rhs=bz[:, i * DO : (i + 1) * DO], start=True, stop=True)
+            nc.scalar.copy(out=bias[:, i, :], in_=pb[:])
 
         xg = [keep.tile([P, CH * D], BF16, name="xg%d" % j, align_bytes=64) for j in range(NCH)]
         xc = [keep.tile([P, CH * P], U32, name="xc%d" % j, align_bytes=64) for j in range(NCH)]
@@ -132,12 +134,12 @@ def tile_contractexpand_pa_kernel(tc, inputs_c_e, Ws, bs, out):
             b = sums.tile([P, D], F32, name="s4f", tag="s4f")
             s4f[j] = b
             nc.vector.tensor_tensor(out=b[:], in0=a[:, 0, :], in1=a[:, 1, :], op=ALU.add)
-            a16 = sums.tile([P, 2 * D], BF16, name="s2b", tag="s2b", align_bytes=64)
-            s2b[j] = a16
-            cast(CAST2, a16[:], a[:].rearrange("q g n -> q (g n)"))
             b16 = sums.tile([P, D], BF16, name="s4b", tag="s4b", align_bytes=64)
             s4b[j] = b16
             cast(CAST4, b16[:], b[:])
+            a16 = keep.tile([P, 2 * D], BF16, name="s2b%d" % j, align_bytes=64)
+            s2b[j] = a16
+            cast(CAST2, a16[:], a[:].rearrange("q g n -> q (g n)"))
             if j == 1:
                 c = sums.tile([P, D], F32, name="acc", tag="acc")
                 acc[0] = c
@@ -165,14 +167,8 @@ def tile_contractexpand_pa_kernel(tc, inputs_c_e, Ws, bs, out):
             nc.vector.quantize_mx(out=c[:].bitcast(FP8X4), scales=s[:], in_=src)
             return (c, s)
 
-        def do_quant(j):
+        def quant_x(j):
             nc.vector.quantize_mx(out=xc[j][:].bitcast(FP8X4), scales=xs[j][:], in_=xg[j][:])
-            s4c[j] = quant(s4b[j][:], D, "q4")
-            s2c[j] = quant(s2b[j][:], 2 * D, "q2")
-            if j == 2:
-                s10c[0] = quant(s10b[0][:], D, "q10")
-            if j == 4:
-                s10c[1] = quant(s10b[1][:], D, "q10")
 
         def mx_bias(codes, scales, col, i, dst):
             y = psy.tile([P, DO], F32, name="y", tag="y")
@@ -194,22 +190,40 @@ def tile_contractexpand_pa_kernel(tc, inputs_c_e, Ws, bs, out):
             nc.gpsimd.tensor_scalar(out=dst, in0=src, scalar1=1.0, scalar2=0.0, op0=ALU.mult, op1=ALU.add)
 
         def unit_r4(j):
+            s4c[j] = quant(s4b[j][:], D, "q4")
             ob = outp.tile([P, CH, DO], F32, name="ob", tag="ob")
             mx_bias(s4c[j][0], s4c[j][1], 0, 2, ob[:, 0, :])
             relu_scale(ob[:, 0, :], 4)
-            repeat(ob[:, 1:CH, :], ob[:, 0:1, :].to_broadcast([P, CH - 1, DO]))
-            nc.sync.dma_start(out=out_rows[2, :, j * CH : (j + 1) * CH, :], in_=ob[:])
+            if EXP4[j]:
+                repeat(ob[:, 1:CH, :], ob[:, 0:1, :].to_broadcast([P, CH - 1, DO]))
+                nc.sync.dma_start(out=out_rows[2, :, j * CH : (j + 1) * CH, :], in_=ob[:])
+            else:
+                nc.sync.dma_start(
+                    out=out_rows[2, :, j * CH : (j + 1) * CH, :], in_=ob[:, 0:1, :].to_broadcast([P, CH, DO])
+                )
 
         def unit_r2(j):
+            s2c[j] = quant(s2b[j][:], 2 * D, "q2")
             ob = outp.tile([P, CH, DO], F32, name="ob", tag="ob")
-            ob4 = ob[:].rearrange("p (g j) d -> p g j d", j=2)
-            for g in range(2):
-                mx_bias(s2c[j][0], s2c[j][1], g, 1, ob4[:, g, 0, :])
-            relu_scale(ob4[:, :, 0, :], 2)
-            repeat(ob4[:, :, 1, :], ob4[:, :, 0, :])
-            nc.sync.dma_start(out=out_rows[1, :, j * CH : (j + 1) * CH, :], in_=ob[:])
+            if EXP2:
+                ob4 = ob[:].rearrange("p (g j) d -> p g j d", j=2)
+                for g in range(2):
+                    mx_bias(s2c[j][0], s2c[j][1], g, 1, ob4[:, g, 0, :])
+                relu_scale(ob4[:, :, 0, :], 2)
+                repeat(ob4[:, :, 1, :], ob4[:, :, 0, :])
+                nc.sync.dma_start(out=out_rows[1, :, j * CH : (j + 1) * CH, :], in_=ob[:])
+            else:
+                for g in range(2):
+                    mx_bias(s2c[j][0], s2c[j][1], g, 1, ob[:, g, :])
+                relu_scale(ob[:, 0:2, :], 2)
+                for g in range(2):
+                    row = j * CH + 2 * g
+                    nc.sync.dma_start(
+                        out=out_rows[1, :, row : row + 2, :], in_=ob[:, g : g + 1, :].to_broadcast([P, 2, DO])
+                    )
 
         def unit_r1(j):
+            quant_x(j)
             ob = outp.tile([P, CH, DO], F32, name="ob", tag="ob")
             for t in range(CH):
                 mx_bias(xc[j], xs[j], t, 0, ob[:, t, :])
@@ -217,32 +231,45 @@ def tile_contractexpand_pa_kernel(tc, inputs_c_e, Ws, bs, out):
             nc.sync.dma_start(out=out_rows[0, :, j * CH : (j + 1) * CH, :], in_=ob[:])
 
         def unit_r10(g):
+            s10c[g] = quant(s10b[g][:], D, "q10")
             ob10 = outp10.tile([P, 5, DO], F32, name="ob10", tag="ob10")
             mx_bias(s10c[g][0], s10c[g][1], 0, 3, ob10[:, 0, :])
             relu_scale(ob10[:, 0, :], 10)
-            repeat(ob10[:, 1:5, :], ob10[:, 0:1, :].to_broadcast([P, 4, DO]))
-            for h in range(2):
-                row = 10 * g + 5 * h
-                nc.sync.dma_start(out=out_rows[3, :, row : row + 5, :], in_=ob10[:])
+            if EXP10[g]:
+                repeat(ob10[:, 1:5, :], ob10[:, 0:1, :].to_broadcast([P, 4, DO]))
+                for h in range(2):
+                    row = 10 * g + 5 * h
+                    nc.sync.dma_start(out=out_rows[3, :, row : row + 5, :], in_=ob10[:])
+            else:
+                nc.sync.dma_start(
+                    out=out_rows[3, :, 10 * g : 10 * g + 10, :], in_=ob10[:, 0:1, :].to_broadcast([P, 10, DO])
+                )
 
         tr_x(0)
         prep_w(2)
+        prep_bias(2)
         do_sums(0)
-        prep_bias()
+        unit_r4(0)
+        tr_x(1)
+        do_sums(1)
+        tr_x(2)
+        do_sums(2)
+        prep_w(3)
+        prep_bias(3)
+        unit_r10(0)
+        unit_r4(1)
+        unit_r4(2)
+        tr_x(3)
+        do_sums(3)
+        tr_x(4)
+        do_sums(4)
+        unit_r10(1)
+        unit_r4(3)
+        unit_r4(4)
         prep_w(1)
+        prep_bias(1)
         prep_w(0)
-        do_quant(0)
+        prep_bias(0)
         for j in range(NCH):
-            if j + 1 < NCH:
-                tr_x(j + 1)
-                if j == 0:
-                    prep_w(3)
-                do_sums(j + 1)
-                do_quant(j + 1)
-            unit_r4(j)
-            if j == 2:
-                unit_r10(0)
-            if j == 4:
-                unit_r10(1)
             unit_r2(j)
             unit_r1(j)

@@ -20,12 +20,30 @@ CH = 4
 NCH = T // CH
 SCALES = (1, 2, 4, 10)
 FLOPS = 2 * sum(N // r for r in SCALES) * D * DO
+WIDX = {"1": 0, "2": 1, "4": 2, "z": 3}
+VCOPY = ("x0b",)
 
-CAST2 = "g"
-CAST4 = "g"
-EXP4 = (False, False, False, False, False)
-EXP10 = (False, False)
-EXP2 = False
+ORDER = (
+    "mz", "id", "Lx0a", "Lx0b", "LW2", "Lx1", "Lb", "Lx2", "LW3", "Lx3", "Lx4", "Tx0a",
+    "LW1", "Tx0b", "Cx0a", "LW0", "Cx0b", "Tw2a", "A0", "Tw2b", "Cw2a", "Tx1a", "Cw2b", "H0",
+    "Tx1b", "Cx1a", "Q40", "QW2", "PB2", "Cx1b", "B0", "Tx2a", "A1", "M40", "Cx2a", "Tx2b",
+    "CB2", "PB3", "B1", "Tw3a", "Cx2b", "E40", "K41", "CB3", "Tw3b", "acc0", "R40", "Q41",
+    "A2", "Cw3a", "M41", "S40", "Tx3a", "Cw3b", "Tx3b", "E41", "sz0", "R41", "Qz0", "Cx3a",
+    "QW3", "S41", "Cx3b", "H2", "Mz0", "Tx4a", "Ez0", "Tx4b", "Q42", "Rz0", "A3", "M42",
+    "Cx4a", "Sz0", "Cx4b", "B3", "E42", "K43", "A4", "R42", "S42", "Q43", "B4", "M43",
+    "Tw1a", "acc1", "K44", "Tw1b", "sz1", "Cw1a", "K20", "E43", "PB1", "Cw1b", "Qx0", "R43",
+    "K21", "Qz1", "Q44", "CB1", "Mz1", "S43", "M44", "Ez1", "Tw0a", "K22", "QW1", "Tw0b",
+    "Cw0a", "E44", "PB0", "Cw0b", "K23", "Rz1", "QW0", "CB0", "Q20", "Sz1", "K24", "M20a",
+    "R44", "M20b", "E20a", "M10a", "S44", "M10b", "E20b", "M10c", "M10d", "Q21", "R20", "E10a",
+    "M21a", "E10b", "M21b", "X20", "Qx1", "R10a", "E10c", "M11a", "E10d", "M11b", "S20", "E21a",
+    "M11c", "R10b", "E21b", "M11d", "Q22", "R21", "S10", "E11a", "M22a", "E11b", "M22b", "X21",
+    "Qx2", "R11a", "E11c", "M12a", "E11d", "M12b", "S21", "E22a", "M12c", "R11b", "E22b", "M12d",
+    "Q23", "R22", "S11", "E12a", "M23a", "E12b", "M23b", "X22", "Qx3", "R12a", "E12c", "M13a",
+    "E12d", "M13b", "S22", "E23a", "M13c", "R12b", "E23b", "M13d", "Q24", "R23", "S12", "E13a",
+    "M24a", "E13b", "M24b", "X23", "Qx4", "R13a", "E13c", "M14a", "E13d", "M14b", "S23", "E24a",
+    "M14c", "R13b", "E24b", "M14d", "E14a", "R24", "S13", "E14b", "E14c", "R14a", "X24", "E14d",
+    "R14b", "S24", "S14",
+)
 
 
 def tile_contractexpand_pa_kernel(tc, inputs_c_e, Ws, bs, out):
@@ -36,240 +54,212 @@ def tile_contractexpand_pa_kernel(tc, inputs_c_e, Ws, bs, out):
     out_rows = out.rearrange("(i p t) d -> i p t d", i=4, t=T)
 
     with ExitStack() as ctx:
-        const = ctx.enter_context(tc.tile_pool(name="const", bufs=1))
         keep = ctx.enter_context(tc.tile_pool(name="keep", bufs=1))
-        sums = ctx.enter_context(tc.tile_pool(name="sums", bufs=3))
-        wstage = ctx.enter_context(tc.tile_pool(name="wstage", bufs=2))
-        outp = ctx.enter_context(tc.tile_pool(name="outp", bufs=7))
-        outp10 = ctx.enter_context(tc.tile_pool(name="outp10", bufs=2))
+        outp = ctx.enter_context(tc.tile_pool(name="outp", bufs=6))
         pst = ctx.enter_context(tc.psum_pool(name="pst", bufs=3))
         psy = ctx.enter_context(tc.psum_pool(name="psy", bufs=5))
+        ctx.enter_context(tc.manual_schedule())
 
-        bz = const.tile([P, 4 * DO], BF16, name="bz")
-        nc.vector.memset(bz[:], 0.0)
-        ident = const.tile([P, P], F32, name="ident")
-        make_identity(nc, ident[:])
-        ones = const.tile([P, P], BF16, name="ones")
-        nc.vector.memset(ones[:], 1.0)
-        bias = const.tile([P, 4, DO], F32, name="bias")
-
+        bz = keep.tile([P, 4 * DO], BF16, name="bz")
+        ident = keep.tile([P, P], F32, name="ident")
+        ones = keep.tile([P, P], BF16, name="ones")
+        bias = keep.tile([P, 4, DO], F32, name="bias")
         x_sb = [keep.tile([P, CH * D], BF16, name="x_sb%d" % j) for j in range(NCH)]
         w_sb = [keep.tile([P, 4 * D], BF16, name="w_sb%d" % i) for i in range(4)]
-
-        def load_x(j):
-            nc.sync.dma_start(out=x_sb[j][:], in_=x_rows[:, j * CH * D : (j + 1) * CH * D])
-
-        def load_w(i):
-            nc.sync.dma_start(out=w_sb[i][:], in_=w_rows[i])
-
-        load_x(0)
-        load_w(2)
-        nc.sync.dma_start(out=bz[0:1, :], in_=b_row)
-        load_x(1)
-        load_x(2)
-        load_w(3)
-        load_x(3)
-        load_x(4)
-        load_w(1)
-        load_w(0)
-
-        def prep_bias(i):
-            pb = psy.tile([P, DO], F32, name="pb", tag="y")
-            nc.tensor.matmul(out=pb[:], lhsT=ones[:], rhs=bz[:, i * DO : (i + 1) * DO], start=True, stop=True)
-            nc.scalar.copy(out=bias[:, i, :], in_=pb[:])
-
         xg = [keep.tile([P, CH * D], BF16, name="xg%d" % j, align_bytes=64) for j in range(NCH)]
+        wg = [keep.tile([P, 4 * DO], BF16, name="wg%d" % i, align_bytes=64) for i in range(4)]
         xc = [keep.tile([P, CH * P], U32, name="xc%d" % j, align_bytes=64) for j in range(NCH)]
         xs = [keep.tile([P, CH * P], U8, name="xs%d" % j, align_bytes=64) for j in range(NCH)]
         wc = [keep.tile([P, DO], U32, name="wc%d" % i, align_bytes=64) for i in range(4)]
         ws = [keep.tile([P, DO], U8, name="ws%d" % i, align_bytes=64) for i in range(4)]
+        s2f = [keep.tile([P, 2, D], F32, name="s2f%d" % j) for j in range(NCH)]
+        s4f = dict((j, keep.tile([P, D], F32, name="s4f%d" % j)) for j in (0, 1, 3, 4))
+        acc = [keep.tile([P, D], F32, name="acc%d" % g) for g in range(2)]
+        s2b = [keep.tile([P, 2 * D], BF16, name="s2b%d" % j, align_bytes=64) for j in range(NCH)]
+        s4b = [keep.tile([P, D], BF16, name="s4b%d" % j, align_bytes=64) for j in range(NCH)]
+        szb = [keep.tile([P, D], BF16, name="szb%d" % g, align_bytes=64) for g in range(2)]
+        c2 = [keep.tile([P, 2 * P], U32, name="c2_%d" % j, align_bytes=64) for j in range(NCH)]
+        p2 = [keep.tile([P, 2 * P], U8, name="p2_%d" % j, align_bytes=64) for j in range(NCH)]
+        c4 = [keep.tile([P, P], U32, name="c4_%d" % j, align_bytes=64) for j in range(NCH)]
+        p4 = [keep.tile([P, P], U8, name="p4_%d" % j, align_bytes=64) for j in range(NCH)]
+        cz = [keep.tile([P, P], U32, name="cz_%d" % g, align_bytes=64) for g in range(2)]
+        pz = [keep.tile([P, P], U8, name="pz_%d" % g, align_bytes=64) for g in range(2)]
+        row4 = [keep.tile([P, 1, DO], F32, name="row4_%d" % j) for j in range(NCH)]
+        rowz = [keep.tile([P, 1, DO], F32, name="rowz_%d" % g) for g in range(2)]
+        banks = {}
+        ys = {}
+        obs = {}
 
-        def prep_w(i):
-            w32 = w_sb[i][:].bitcast(F32)
-            wg = wstage.tile([P, 4 * DO], BF16, name="wg", tag="wg", align_bytes=64)
-            wg32 = wg[:].bitcast(F32).rearrange("q (p h m) -> q p h m", h=2, m=4)
-            for h in range(2):
-                pt = pst.tile([P, 512], F32, name="pt", tag="pt")
-                for m in range(4):
-                    nc.tensor.transpose(
-                        pt[:, m * P : (m + 1) * P], w32[:, (4 * h + m) * P : (4 * h + m + 1) * P], ident[:]
-                    )
-                nc.scalar.copy(out=wg32[:, :, h, :], in_=pt[:].rearrange("q (m p) -> q p m", m=4))
-            nc.vector.quantize_mx(out=wc[i][:].bitcast(FP8X4), scales=ws[i][:], in_=wg[:])
+        def add(dst, a, b):
+            nc.vector.tensor_tensor(out=dst, in0=a, in1=b, op=ALU.add)
 
-        def tr_x(j):
-            x32 = x_sb[j][:].bitcast(F32)
-            xg32 = xg[j][:].bitcast(F32).rearrange("q (t p u) -> q t p u", t=CH, u=2)
-            for h in range(2):
-                pt = pst.tile([P, 512], F32, name="pt", tag="pt")
-                for m in range(4):
-                    nc.tensor.transpose(
-                        pt[:, m * P : (m + 1) * P], x32[:, (4 * h + m) * P : (4 * h + m + 1) * P], ident[:]
-                    )
-                nc.scalar.copy(
-                    out=xg32[:, 2 * h : 2 * h + 2, :, :],
-                    in_=pt[:].rearrange("q (t u p) -> q t p u", t=2, u=2),
-                )
-
-        def cast(eng, dst, src):
-            if eng == "g":
-                nc.gpsimd.tensor_scalar(out=dst, in0=src, scalar1=1.0, scalar2=0.0, op0=ALU.mult, op1=ALU.add)
-            elif eng == "s":
-                nc.scalar.copy(out=dst, in_=src)
-            else:
-                nc.vector.tensor_copy(out=dst, in_=src)
-
-        s2f = {}
-        s4f = {}
-        acc = {}
-        s2b = {}
-        s4b = {}
-        s10b = {}
-
-        def do_sums(j):
-            xg4 = xg[j][:].rearrange("q (g j n) -> q g j n", g=2, j=2)
-            a = sums.tile([P, 2, D], F32, name="s2f", tag="s2f")
-            s2f[j] = a
-            nc.vector.tensor_tensor(out=a[:], in0=xg4[:, :, 0, :], in1=xg4[:, :, 1, :], op=ALU.add)
-            b = sums.tile([P, D], F32, name="s4f", tag="s4f")
-            s4f[j] = b
-            nc.vector.tensor_tensor(out=b[:], in0=a[:, 0, :], in1=a[:, 1, :], op=ALU.add)
-            b16 = sums.tile([P, D], BF16, name="s4b", tag="s4b", align_bytes=64)
-            s4b[j] = b16
-            cast(CAST4, b16[:], b[:])
-            a16 = keep.tile([P, 2 * D], BF16, name="s2b%d" % j, align_bytes=64)
-            s2b[j] = a16
-            cast(CAST2, a16[:], a[:].rearrange("q g n -> q (g n)"))
-            if j == 1:
-                c = sums.tile([P, D], F32, name="acc", tag="acc")
-                acc[0] = c
-                nc.vector.tensor_tensor(out=c[:], in0=s4f[0][:], in1=s4f[1][:], op=ALU.add)
-            if j == 2:
-                c16 = sums.tile([P, D], BF16, name="s10b", tag="s10b", align_bytes=64)
-                s10b[0] = c16
-                nc.vector.tensor_tensor(out=c16[:], in0=acc[0][:], in1=a[:, 0, :], op=ALU.add)
-            if j == 3:
-                c = sums.tile([P, D], F32, name="acc", tag="acc")
-                acc[1] = c
-                nc.vector.tensor_tensor(out=c[:], in0=s2f[2][:, 1, :], in1=b[:], op=ALU.add)
-            if j == 4:
-                c16 = sums.tile([P, D], BF16, name="s10b", tag="s10b", align_bytes=64)
-                s10b[1] = c16
-                nc.vector.tensor_tensor(out=c16[:], in0=acc[1][:], in1=b[:], op=ALU.add)
-
-        s2c = {}
-        s4c = {}
-        s10c = {}
-
-        def quant(src, width, tagname):
-            c = sums.tile([P, width // 4], U32, name=tagname + "c", tag=tagname + "c", align_bytes=64)
-            s = sums.tile([P, width // 4], U8, name=tagname + "s", tag=tagname + "s", align_bytes=64)
-            nc.vector.quantize_mx(out=c[:].bitcast(FP8X4), scales=s[:], in_=src)
-            return (c, s)
-
-        def quant_x(j):
-            nc.vector.quantize_mx(out=xc[j][:].bitcast(FP8X4), scales=xs[j][:], in_=xg[j][:])
-
-        def mx_bias(codes, scales, col, i, dst):
-            y = psy.tile([P, DO], F32, name="y", tag="y")
-            nc.tensor.matmul_mx(
-                out=y[:],
-                lhsT=codes[:, col * P : (col + 1) * P].bitcast(FP8X4),
-                lhsT_scale=scales[:, col * P : (col + 1) * P],
-                rhs=wc[i][:].bitcast(FP8X4),
-                rhs_scale=ws[i][:],
-                start=True,
-                stop=True,
-            )
-            nc.vector.tensor_tensor(out=dst, in0=y[:], in1=bias[:, i, :], op=ALU.add)
-
-        def relu_scale(rows, r):
-            nc.scalar.activation(out=rows, in_=rows, func=ACT.Relu, scale=1.0 / r)
-
-        def repeat(dst, src):
+        def gcopy(dst, src):
             nc.gpsimd.tensor_scalar(out=dst, in0=src, scalar1=1.0, scalar2=0.0, op0=ALU.mult, op1=ALU.add)
 
-        def unit_r4(j):
-            s4c[j] = quant(s4b[j][:], D, "q4")
-            ob = outp.tile([P, CH, DO], F32, name="ob", tag="ob")
-            mx_bias(s4c[j][0], s4c[j][1], 0, 2, ob[:, 0, :])
-            relu_scale(ob[:, 0, :], 4)
-            if EXP4[j]:
-                repeat(ob[:, 1:CH, :], ob[:, 0:1, :].to_broadcast([P, CH - 1, DO]))
-                nc.sync.dma_start(out=out_rows[2, :, j * CH : (j + 1) * CH, :], in_=ob[:])
-            else:
-                nc.sync.dma_start(
-                    out=out_rows[2, :, j * CH : (j + 1) * CH, :], in_=ob[:, 0:1, :].to_broadcast([P, CH, DO])
+        def quant(codes, plane, src):
+            nc.vector.quantize_mx(out=codes.bitcast(FP8X4), scales=plane, in_=src)
+
+        def operand(t):
+            n = int(t[1])
+            col = "abcd".index(t[2]) if len(t) > 2 else 0
+            if t[0] == "1":
+                return xc[n], xs[n], col
+            if t[0] == "2":
+                return c2[n], p2[n], col
+            if t[0] == "4":
+                return c4[n], p4[n], 0
+            return cz[n], pz[n], 0
+
+        def dest(t):
+            n = int(t[1])
+            if t[0] == "4":
+                return row4[n][:, 0, :]
+            if t[0] == "z":
+                return rowz[n][:, 0, :]
+            u = t[0:2]
+            if u not in obs:
+                ob = outp.tile([P, CH, DO], F32, name="ob", tag="ob")
+                obs[u] = ob
+            col = "abcd".index(t[2])
+            if t[0] == "2":
+                return obs[u][:, 2 * col, :]
+            return obs[u][:, col, :]
+
+        def relu(rows, r):
+            nc.scalar.activation(out=rows, in_=rows, func=ACT.Relu, scale=1.0 / r)
+
+        def emit(op):
+            k = op[0]
+            a = op[1:]
+            if op == "mz":
+                nc.vector.memset(bz[:], 0.0)
+                nc.vector.memset(ones[:], 1.0)
+            elif op == "id":
+                make_identity(nc, ident[:])
+            elif op == "Lb":
+                nc.sync.dma_start(out=bz[0:1, :], in_=b_row)
+            elif op[0:2] == "Lx":
+                j = int(op[2])
+                lo = 0
+                hi = CH * D
+                if len(op) > 3:
+                    lo = "ab".index(op[3]) * 2 * D
+                    hi = lo + 2 * D
+                nc.sync.dma_start(out=x_sb[j][:, lo:hi], in_=x_rows[:, j * CH * D + lo : j * CH * D + hi])
+            elif op[0:2] == "LW":
+                i = int(op[2])
+                nc.sync.dma_start(out=w_sb[i][:], in_=w_rows[i])
+            elif k == "T":
+                src = (x_sb if a[0] == "x" else w_sb)[int(a[1])][:].bitcast(F32)
+                h = "ab".index(a[2])
+                pt = pst.tile([P, 512], F32, name="pt", tag="pt")
+                banks[a] = pt
+                for m in range(4):
+                    nc.tensor.transpose(pt[:, m * P : (m + 1) * P], src[:, (4 * h + m) * P : (4 * h + m + 1) * P], ident[:])
+            elif op[0:2] == "CB":
+                i = int(op[2])
+                nc.scalar.copy(out=bias[:, i, :], in_=ys["b" + op[2]][:])
+            elif k == "C":
+                n = int(a[1])
+                h = "ab".index(a[2])
+                pt = banks[a]
+                if a[0] == "x":
+                    dst = xg[n][:].bitcast(F32).rearrange("q (t p u) -> q t p u", t=CH, u=2)[:, 2 * h : 2 * h + 2, :, :]
+                    src = pt[:].rearrange("q (t u p) -> q t p u", t=2, u=2)
+                else:
+                    dst = wg[n][:].bitcast(F32).rearrange("q (p h m) -> q p h m", h=2, m=4)[:, :, h, :]
+                    src = pt[:].rearrange("q (m p) -> q p m", m=4)
+                if a in VCOPY:
+                    nc.vector.tensor_copy(out=dst, in_=src)
+                else:
+                    nc.scalar.copy(out=dst, in_=src)
+            elif op[0:2] == "PB":
+                i = int(op[2])
+                pb = psy.tile([P, DO], F32, name="pb", tag="y")
+                ys["b" + op[2]] = pb
+                nc.tensor.matmul(out=pb[:], lhsT=ones[:], rhs=bz[:, i * DO : (i + 1) * DO], start=True, stop=True)
+            elif op[0:2] == "QW":
+                i = int(op[2])
+                quant(wc[i][:], ws[i][:], wg[i][:])
+            elif op[0:2] == "Qx":
+                j = int(op[2])
+                quant(xc[j][:], xs[j][:], xg[j][:])
+            elif op[0:2] == "Q2":
+                j = int(op[2])
+                quant(c2[j][:], p2[j][:], s2b[j][:])
+            elif op[0:2] == "Q4":
+                j = int(op[2])
+                quant(c4[j][:], p4[j][:], s4b[j][:])
+            elif op[0:2] == "Qz":
+                g = int(op[2])
+                quant(cz[g][:], pz[g][:], szb[g][:])
+            elif k == "A":
+                j = int(a)
+                xg4 = xg[j][:].rearrange("q (g j n) -> q g j n", g=2, j=2)
+                add(s2f[j][:], xg4[:, :, 0, :], xg4[:, :, 1, :])
+            elif k == "B":
+                j = int(a)
+                add(s4f[j][:], s2f[j][:, 0, :], s2f[j][:, 1, :])
+            elif k == "H":
+                j = int(a)
+                add(s4b[j][:], s2f[j][:, 0, :], s2f[j][:, 1, :])
+            elif op == "acc0":
+                add(acc[0][:], s4f[0][:], s4f[1][:])
+            elif op == "sz0":
+                add(szb[0][:], acc[0][:], s2f[2][:, 0, :])
+            elif op == "acc1":
+                add(acc[1][:], s2f[2][:, 1, :], s4f[3][:])
+            elif op == "sz1":
+                add(szb[1][:], acc[1][:], s4f[4][:])
+            elif op[0:2] == "K4":
+                j = int(op[2])
+                gcopy(s4b[j][:], s4f[j][:])
+            elif op[0:2] == "K2":
+                j = int(op[2])
+                gcopy(s2b[j][:], s2f[j][:].rearrange("q g n -> q (g n)"))
+            elif k == "M":
+                codes, plane, col = operand(a)
+                i = WIDX[a[0]]
+                y = psy.tile([P, DO], F32, name="y", tag="y")
+                ys[a] = y
+                nc.tensor.matmul_mx(
+                    out=y[:],
+                    lhsT=codes[:, col * P : (col + 1) * P].bitcast(FP8X4),
+                    lhsT_scale=plane[:, col * P : (col + 1) * P],
+                    rhs=wc[i][:].bitcast(FP8X4),
+                    rhs_scale=ws[i][:],
+                    start=True,
+                    stop=True,
                 )
-
-        def unit_r2(j):
-            s2c[j] = quant(s2b[j][:], 2 * D, "q2")
-            ob = outp.tile([P, CH, DO], F32, name="ob", tag="ob")
-            if EXP2:
-                ob4 = ob[:].rearrange("p (g j) d -> p g j d", j=2)
-                for g in range(2):
-                    mx_bias(s2c[j][0], s2c[j][1], g, 1, ob4[:, g, 0, :])
-                relu_scale(ob4[:, :, 0, :], 2)
-                repeat(ob4[:, :, 1, :], ob4[:, :, 0, :])
-                nc.sync.dma_start(out=out_rows[1, :, j * CH : (j + 1) * CH, :], in_=ob[:])
+            elif k == "E":
+                add(dest(a), ys[a][:], bias[:, WIDX[a[0]], :])
+            elif k == "R":
+                n = int(a[1])
+                if a[0] == "4":
+                    relu(row4[n][:], 4)
+                elif a[0] == "z":
+                    relu(rowz[n][:], 10)
+                elif a[0] == "2":
+                    relu(obs[a[0:2]][:].rearrange("p (g j) d -> p g j d", j=2)[:, :, 0, :], 2)
+                else:
+                    h = "ab".index(a[2])
+                    relu(obs[a[0:2]][:, 2 * h : 2 * h + 2, :], 1)
+            elif op[0:2] == "X2":
+                ob4 = obs[a][:].rearrange("p (g j) d -> p g j d", j=2)
+                gcopy(ob4[:, :, 1, :], ob4[:, :, 0, :])
+            elif k == "S":
+                n = int(a[1])
+                if a[0] == "4":
+                    nc.sync.dma_start(out=out_rows[2, :, n * CH : (n + 1) * CH, :], in_=row4[n][:].to_broadcast([P, CH, DO]))
+                elif a[0] == "z":
+                    row = 10 * n
+                    for cnt in (4, 4, 2):
+                        nc.sync.dma_start(out=out_rows[3, :, row : row + cnt, :], in_=rowz[n][:].to_broadcast([P, cnt, DO]))
+                        row += cnt
+                else:
+                    nc.sync.dma_start(out=out_rows[WIDX[a[0]], :, n * CH : (n + 1) * CH, :], in_=obs[a][:])
             else:
-                for g in range(2):
-                    mx_bias(s2c[j][0], s2c[j][1], g, 1, ob[:, g, :])
-                relu_scale(ob[:, 0:2, :], 2)
-                for g in range(2):
-                    row = j * CH + 2 * g
-                    nc.sync.dma_start(
-                        out=out_rows[1, :, row : row + 2, :], in_=ob[:, g : g + 1, :].to_broadcast([P, 2, DO])
-                    )
+                raise ValueError(op)
 
-        def unit_r1(j):
-            quant_x(j)
-            ob = outp.tile([P, CH, DO], F32, name="ob", tag="ob")
-            for t in range(CH):
-                mx_bias(xc[j], xs[j], t, 0, ob[:, t, :])
-            relu_scale(ob[:], 1)
-            nc.sync.dma_start(out=out_rows[0, :, j * CH : (j + 1) * CH, :], in_=ob[:])
-
-        def unit_r10(g):
-            s10c[g] = quant(s10b[g][:], D, "q10")
-            ob10 = outp10.tile([P, 5, DO], F32, name="ob10", tag="ob10")
-            mx_bias(s10c[g][0], s10c[g][1], 0, 3, ob10[:, 0, :])
-            relu_scale(ob10[:, 0, :], 10)
-            if EXP10[g]:
-                repeat(ob10[:, 1:5, :], ob10[:, 0:1, :].to_broadcast([P, 4, DO]))
-                for h in range(2):
-                    row = 10 * g + 5 * h
-                    nc.sync.dma_start(out=out_rows[3, :, row : row + 5, :], in_=ob10[:])
-            else:
-                nc.sync.dma_start(
-                    out=out_rows[3, :, 10 * g : 10 * g + 10, :], in_=ob10[:, 0:1, :].to_broadcast([P, 10, DO])
-                )
-
-        tr_x(0)
-        prep_w(2)
-        prep_bias(2)
-        do_sums(0)
-        unit_r4(0)
-        tr_x(1)
-        do_sums(1)
-        tr_x(2)
-        do_sums(2)
-        prep_w(3)
-        prep_bias(3)
-        unit_r10(0)
-        unit_r4(1)
-        unit_r4(2)
-        tr_x(3)
-        do_sums(3)
-        tr_x(4)
-        do_sums(4)
-        unit_r10(1)
-        unit_r4(3)
-        unit_r4(4)
-        prep_w(1)
-        prep_bias(1)
-        prep_w(0)
-        prep_bias(0)
-        for j in range(NCH):
-            unit_r2(j)
-            unit_r1(j)
+        for op in ORDER:
+            emit(op)

@@ -21,23 +21,24 @@ NCH = T // CH
 SCALES = (1, 2, 4, 10)
 FLOPS = 2 * sum(N // r for r in SCALES) * D * DO
 WIDX = {"1": 0, "2": 1, "4": 2, "z": 3}
+FULL = ("42", "43", "44", "z1",)
 VCOPY = ("x0b",)
 
 ORDER = (
-    "mz", "id", "Lx0a", "Lx0b", "LW2", "Lx1", "Lb", "Lx2", "LW3", "Lx3", "Lx4", "Tx0a",
-    "LW1", "Tx0b", "Cx0a", "LW0", "Cx0b", "Tw2a", "A0", "Tw2b", "Cw2a", "Tx1a", "Cw2b", "H0",
-    "Tx1b", "Cx1a", "Q40", "QW2", "PB2", "Cx1b", "B0", "Tx2a", "A1", "M40", "Cx2a", "Tx2b",
-    "CB2", "PB3", "B1", "Tw3a", "Cx2b", "E40", "K41", "CB3", "Tw3b", "acc0", "R40", "Q41",
-    "A2", "Cw3a", "M41", "S40", "Tx3a", "Cw3b", "Tx3b", "E41", "sz0", "R41", "Qz0", "Cx3a",
-    "QW3", "S41", "Cx3b", "H2", "Mz0", "Tx4a", "Ez0", "Tx4b", "Q42", "Rz0", "A3", "M42",
-    "Cx4a", "Sz0", "Cx4b", "B3", "E42", "K43", "A4", "R42", "S42", "Q43", "B4", "M43",
-    "Tw1a", "acc1", "K44", "Tw1b", "sz1", "Cw1a", "K20", "E43", "PB1", "Cw1b", "Qx0", "R43",
-    "K21", "Qz1", "Q44", "CB1", "Mz1", "S43", "M44", "Ez1", "Tw0a", "K22", "QW1", "Tw0b",
-    "Cw0a", "E44", "PB0", "Cw0b", "K23", "Rz1", "QW0", "CB0", "Q20", "Sz1", "K24", "M20a",
-    "R44", "M20b", "E20a", "M10a", "S44", "M10b", "E20b", "M10c", "M10d", "Q21", "R20", "E10a",
-    "M21a", "E10b", "M21b", "X20", "Qx1", "R10a", "E10c", "M11a", "E10d", "M11b", "S20", "E21a",
-    "M11c", "R10b", "E21b", "M11d", "Q22", "R21", "S10", "E11a", "M22a", "E11b", "M22b", "X21",
-    "Qx2", "R11a", "E11c", "M12a", "E11d", "M12b", "S21", "E22a", "M12c", "R11b", "E22b", "M12d",
+    "mz", "id", "Lx0a", "Lx0b", "LW2", "Lx1", "Lx2", "Lb", "LW3", "Lx3", "Lx4", "Tx0a",
+    "Tx0b", "Cx0a", "Cx0b", "Tw2a", "A0", "Tw2b", "Cw2a", "Tx1a", "Cw2b", "LW1", "H0", "Tx1b",
+    "Cx1a", "Q40", "B0", "PB2", "Cx1b", "QW2", "Tx2a", "CB2", "A1", "Tx2b", "Cx2a", "M40",
+    "Cx2b", "PB3", "B1", "Tw3a", "E40", "K41", "Tw3b", "Cw3a", "acc0", "Tx3a", "CB3", "Q41",
+    "LW0", "A2", "R40", "M41", "Tx3b", "Cw3b", "S40", "E41", "Cx3a", "Tx4a", "QW3", "Cx3b",
+    "Tx4b", "sz0", "R41", "Qz0", "H2", "Mz0", "Cx4a", "S41", "Tw1a", "Q42", "Cx4b", "Ez0",
+    "M42", "A3", "Tw1b", "Rz0", "Tw0a", "Cw1a", "Sz0", "B3", "Cw1b", "E42", "K43", "Cw0a",
+    "A4", "R42", "Q43", "B4", "M43", "acc1", "K44", "E43", "S42", "K20", "sz1", "R43",
+    "Qz1", "Mz1", "K21", "Tw0b", "Ez1", "Q44", "QW1", "M44", "K22", "Rz1", "PB1", "S43",
+    "Qx0", "PB0", "Q20", "E44", "M20a", "K23", "M20b", "K24", "Cw0b", "Sz1", "CB1", "QW0",
+    "CB0", "E20a", "M10a", "M10b", "R44", "E20b", "M10c", "M10d", "Q21", "E10a", "M21a", "E10b",
+    "M21b", "Qx1", "R20", "S44", "E10c", "M11a", "E10d", "R10a", "M11b", "X20", "E21a", "M11c",
+    "E21b", "R10b", "M11d", "S20", "Q22", "E11a", "M22a", "R21", "S10", "E11b", "M22b", "Qx2",
+    "R11a", "X21", "E11c", "M12a", "E11d", "M12b", "E22a", "S21", "M12c", "R11b", "E22b", "M12d",
     "Q23", "R22", "S11", "E12a", "M23a", "E12b", "M23b", "X22", "Qx3", "R12a", "E12c", "M13a",
     "E12d", "M13b", "S22", "E23a", "M13c", "R12b", "E23b", "M13d", "Q24", "R23", "S12", "E13a",
     "M24a", "E13b", "M24b", "X23", "Qx4", "R13a", "E13c", "M14a", "E13d", "M14b", "S23", "E24a",
@@ -55,6 +56,7 @@ def tile_contractexpand_pa_kernel(tc, inputs_c_e, Ws, bs, out):
 
     with ExitStack() as ctx:
         keep = ctx.enter_context(tc.tile_pool(name="keep", bufs=1))
+        wpool = ctx.enter_context(tc.tile_pool(name="wpool", bufs=2))
         outp = ctx.enter_context(tc.tile_pool(name="outp", bufs=6))
         pst = ctx.enter_context(tc.psum_pool(name="pst", bufs=3))
         psy = ctx.enter_context(tc.psum_pool(name="psy", bufs=5))
@@ -65,7 +67,7 @@ def tile_contractexpand_pa_kernel(tc, inputs_c_e, Ws, bs, out):
         ones = keep.tile([P, P], BF16, name="ones")
         bias = keep.tile([P, 4, DO], F32, name="bias")
         x_sb = [keep.tile([P, CH * D], BF16, name="x_sb%d" % j) for j in range(NCH)]
-        w_sb = [keep.tile([P, 4 * D], BF16, name="w_sb%d" % i) for i in range(4)]
+        w_sb = {}
         xg = [keep.tile([P, CH * D], BF16, name="xg%d" % j, align_bytes=64) for j in range(NCH)]
         wg = [keep.tile([P, 4 * DO], BF16, name="wg%d" % i, align_bytes=64) for i in range(4)]
         xc = [keep.tile([P, CH * P], U32, name="xc%d" % j, align_bytes=64) for j in range(NCH)]
@@ -86,6 +88,7 @@ def tile_contractexpand_pa_kernel(tc, inputs_c_e, Ws, bs, out):
         pz = [keep.tile([P, P], U8, name="pz_%d" % g, align_bytes=64) for g in range(2)]
         row4 = [keep.tile([P, 1, DO], F32, name="row4_%d" % j) for j in range(NCH)]
         rowz = [keep.tile([P, 1, DO], F32, name="rowz_%d" % g) for g in range(2)]
+        obz = keep.tile([P, 5, DO], F32, name="obz")
         banks = {}
         ys = {}
         obs = {}
@@ -148,7 +151,9 @@ def tile_contractexpand_pa_kernel(tc, inputs_c_e, Ws, bs, out):
                 nc.sync.dma_start(out=x_sb[j][:, lo:hi], in_=x_rows[:, j * CH * D + lo : j * CH * D + hi])
             elif op[0:2] == "LW":
                 i = int(op[2])
-                nc.sync.dma_start(out=w_sb[i][:], in_=w_rows[i])
+                w_in = wpool.tile([P, 4 * D], BF16, name="w_in", tag="w_in")
+                w_sb[i] = w_in
+                nc.sync.dma_start(out=w_in[:], in_=w_rows[i])
             elif k == "T":
                 src = (x_sb if a[0] == "x" else w_sb)[int(a[1])][:].bitcast(F32)
                 h = "ab".index(a[2])
@@ -235,7 +240,13 @@ def tile_contractexpand_pa_kernel(tc, inputs_c_e, Ws, bs, out):
                 add(dest(a), ys[a][:], bias[:, WIDX[a[0]], :])
             elif k == "R":
                 n = int(a[1])
-                if a[0] == "4":
+                if a[0] == "4" and a in FULL:
+                    ob = outp.tile([P, CH, DO], F32, name="ob", tag="ob")
+                    obs[a] = ob
+                    nc.scalar.activation(out=ob[:], in_=row4[n][:].to_broadcast([P, CH, DO]), func=ACT.Relu, scale=0.25)
+                elif a[0] == "z" and a in FULL:
+                    nc.scalar.activation(out=obz[:], in_=rowz[n][:].to_broadcast([P, 5, DO]), func=ACT.Relu, scale=0.1)
+                elif a[0] == "4":
                     relu(row4[n][:], 4)
                 elif a[0] == "z":
                     relu(rowz[n][:], 10)
@@ -249,7 +260,11 @@ def tile_contractexpand_pa_kernel(tc, inputs_c_e, Ws, bs, out):
                 gcopy(ob4[:, :, 1, :], ob4[:, :, 0, :])
             elif k == "S":
                 n = int(a[1])
-                if a[0] == "4":
+                if a[0] == "z" and a in FULL:
+                    for h in range(2):
+                        row = 10 * n + 5 * h
+                        nc.sync.dma_start(out=out_rows[3, :, row : row + 5, :], in_=obz[:])
+                elif a[0] == "4" and a not in FULL:
                     nc.sync.dma_start(out=out_rows[2, :, n * CH : (n + 1) * CH, :], in_=row4[n][:].to_broadcast([P, CH, DO]))
                 elif a[0] == "z":
                     row = 10 * n

@@ -8,273 +8,285 @@ BF16 = mybir.dt.bfloat16
 U32 = mybir.dt.uint32
 U8 = mybir.dt.uint8
 FP8X4 = mybir.dt.float8_e4m3fn_x4
-ALU = mybir.AluOpType
-ACT = mybir.ActivationFunctionType
+ADD = mybir.AluOpType.add
+MULT = mybir.AluOpType.mult
+RELU = mybir.ActivationFunctionType.Relu
 
 P = 128
-N = 2560
-D = 512
-DO = 512
-T = N // P
-CH = 4
-NCH = T // CH
-SCALES = (1, 2, 4, 10)
-FLOPS = 2 * sum(N // r for r in SCALES) * D * DO
-WIDX = {"1": 0, "2": 1, "4": 2, "z": 3}
-FULL = ("42", "43", "44", "z1",)
-VCOPY = ("x0b",)
-
-ORDER = (
-    "mz", "id", "Lx0a", "Lx0b", "LW2", "Lx1", "Lx2", "Lb", "LW3", "Lx3", "Lx4", "Tx0a",
-    "Tx0b", "Cx0a", "Cx0b", "Tw2a", "A0", "Tw2b", "Cw2a", "Tx1a", "Cw2b", "LW1", "H0", "Tx1b",
-    "Cx1a", "Q40", "B0", "PB2", "Cx1b", "QW2", "Tx2a", "CB2", "A1", "Tx2b", "Cx2a", "M40",
-    "Cx2b", "PB3", "B1", "Tw3a", "E40", "K41", "Tw3b", "Cw3a", "acc0", "Tx3a", "CB3", "Q41",
-    "LW0", "A2", "R40", "M41", "Tx3b", "Cw3b", "S40", "E41", "Cx3a", "Tx4a", "QW3", "Cx3b",
-    "Tx4b", "sz0", "R41", "Qz0", "H2", "Mz0", "Cx4a", "S41", "Tw1a", "Q42", "Cx4b", "Ez0",
-    "M42", "A3", "Tw1b", "Rz0", "Tw0a", "Cw1a", "Sz0", "B3", "Cw1b", "E42", "K43", "Cw0a",
-    "A4", "R42", "Q43", "B4", "M43", "acc1", "K44", "E43", "S42", "K20", "sz1", "R43",
-    "Qz1", "Mz1", "K21", "Tw0b", "Ez1", "Q44", "QW1", "M44", "K22", "Rz1", "PB1", "S43",
-    "Qx0", "PB0", "Q20", "E44", "M20a", "K23", "M20b", "K24", "Cw0b", "Sz1", "CB1", "QW0",
-    "CB0", "E20a", "M10a", "M10b", "R44", "E20b", "M10c", "M10d", "Q21", "E10a", "M21a", "E10b",
-    "M21b", "Qx1", "R20", "S44", "E10c", "M11a", "E10d", "R10a", "M11b", "X20", "E21a", "M11c",
-    "E21b", "R10b", "M11d", "S20", "Q22", "E11a", "M22a", "R21", "S10", "E11b", "M22b", "Qx2",
-    "R11a", "X21", "E11c", "M12a", "E11d", "M12b", "E22a", "S21", "M12c", "R11b", "E22b", "M12d",
-    "Q23", "R22", "S11", "E12a", "M23a", "E12b", "M23b", "X22", "Qx3", "R12a", "E12c", "M13a",
-    "E12d", "M13b", "S22", "E23a", "M13c", "R12b", "E23b", "M13d", "Q24", "R23", "S12", "E13a",
-    "M24a", "E13b", "M24b", "X23", "Qx4", "R13a", "E13c", "M14a", "E13d", "M14b", "S23", "E24a",
-    "M14c", "R13b", "E24b", "M14d", "E14a", "R24", "S13", "E14b", "E14c", "R14a", "X24", "E14d",
-    "R14b", "S24", "S14",
-)
+ROWS = 2560
+K = 512
+OUT = 512
+GROUP = (1, 2, 4, 10)
+TILES = ROWS // P
+CHUNK = 4
+CHUNKS = TILES // CHUNK
+PSUM_BANK = 512
+PRODUCT_BANKS = 5
+FLOPS = 2 * sum(ROWS // r for r in GROUP) * K * OUT
 
 
 def tile_contractexpand_pa_kernel(tc, inputs_c_e, Ws, bs, out):
     nc = tc.nc
-    x_rows = inputs_c_e.rearrange("(p t) k -> p (t k)", t=T)
+    x_rows = inputs_c_e.rearrange("(p t) k -> p (t k)", t=TILES)
     w_rows = Ws.rearrange("i (p c) k -> i p (c k)", c=4)
-    b_row = bs.rearrange("(o i) d -> o (i d)", o=1)
-    out_rows = out.rearrange("(i p t) d -> i p t d", i=4, t=T)
+    bias_row = bs.rearrange("(o i) d -> o (i d)", o=1)
+    out_rows = out.rearrange("(i p t) d -> i p t d", i=len(GROUP), t=TILES)
 
     with ExitStack() as ctx:
         keep = ctx.enter_context(tc.tile_pool(name="keep", bufs=1))
-        wpool = ctx.enter_context(tc.tile_pool(name="wpool", bufs=2))
-        outp = ctx.enter_context(tc.tile_pool(name="outp", bufs=6))
-        pst = ctx.enter_context(tc.psum_pool(name="pst", bufs=3))
-        psy = ctx.enter_context(tc.psum_pool(name="psy", bufs=5))
+        w_pool = ctx.enter_context(tc.tile_pool(name="w_pool", bufs=2))
+        out_pool = ctx.enter_context(tc.tile_pool(name="out_pool", bufs=6))
+        flip_pool = ctx.enter_context(tc.psum_pool(name="flip_pool", bufs=8 - PRODUCT_BANKS))
+        product_pool = ctx.enter_context(tc.psum_pool(name="product_pool", bufs=PRODUCT_BANKS))
         ctx.enter_context(tc.manual_schedule())
 
-        bz = keep.tile([P, 4 * DO], BF16, name="bz")
-        ident = keep.tile([P, P], F32, name="ident")
+        identity = keep.tile([P, P], F32, name="identity")
         ones = keep.tile([P, P], BF16, name="ones")
-        bias = keep.tile([P, 4, DO], F32, name="bias")
-        x_sb = [keep.tile([P, CH * D], BF16, name="x_sb%d" % j) for j in range(NCH)]
-        w_sb = {}
-        xg = [keep.tile([P, CH * D], BF16, name="xg%d" % j, align_bytes=64) for j in range(NCH)]
-        wg = [keep.tile([P, 4 * DO], BF16, name="wg%d" % i, align_bytes=64) for i in range(4)]
-        xc = [keep.tile([P, CH * P], U32, name="xc%d" % j, align_bytes=64) for j in range(NCH)]
-        xs = [keep.tile([P, CH * P], U8, name="xs%d" % j, align_bytes=64) for j in range(NCH)]
-        wc = [keep.tile([P, DO], U32, name="wc%d" % i, align_bytes=64) for i in range(4)]
-        ws = [keep.tile([P, DO], U8, name="ws%d" % i, align_bytes=64) for i in range(4)]
-        s2f = [keep.tile([P, 2, D], F32, name="s2f%d" % j) for j in range(NCH)]
-        s4f = dict((j, keep.tile([P, D], F32, name="s4f%d" % j)) for j in (0, 1, 3, 4))
-        acc = [keep.tile([P, D], F32, name="acc%d" % g) for g in range(2)]
-        s2b = [keep.tile([P, 2 * D], BF16, name="s2b%d" % j, align_bytes=64) for j in range(NCH)]
-        s4b = [keep.tile([P, D], BF16, name="s4b%d" % j, align_bytes=64) for j in range(NCH)]
-        szb = [keep.tile([P, D], BF16, name="szb%d" % g, align_bytes=64) for g in range(2)]
-        c2 = [keep.tile([P, 2 * P], U32, name="c2_%d" % j, align_bytes=64) for j in range(NCH)]
-        p2 = [keep.tile([P, 2 * P], U8, name="p2_%d" % j, align_bytes=64) for j in range(NCH)]
-        c4 = [keep.tile([P, P], U32, name="c4_%d" % j, align_bytes=64) for j in range(NCH)]
-        p4 = [keep.tile([P, P], U8, name="p4_%d" % j, align_bytes=64) for j in range(NCH)]
-        cz = [keep.tile([P, P], U32, name="cz_%d" % g, align_bytes=64) for g in range(2)]
-        pz = [keep.tile([P, P], U8, name="pz_%d" % g, align_bytes=64) for g in range(2)]
-        row4 = [keep.tile([P, 1, DO], F32, name="row4_%d" % j) for j in range(NCH)]
-        rowz = [keep.tile([P, 1, DO], F32, name="rowz_%d" % g) for g in range(2)]
-        obz = keep.tile([P, 5, DO], F32, name="obz")
-        banks = {}
-        ys = {}
-        obs = {}
+        bias_in = keep.tile([P, len(GROUP) * OUT], BF16, name="bias_in")
+        bias = keep.tile([P, len(GROUP), OUT], F32, name="bias")
+        x_in = [keep.tile([P, CHUNK * K], BF16, name="x_in%d" % j) for j in range(CHUNKS)]
+        w_in = {}
+        x_t = [keep.tile([P, CHUNK * K], BF16, name="x_t%d" % j, align_bytes=64) for j in range(CHUNKS)]
+        w_t = [keep.tile([P, 4 * OUT], BF16, name="w_t%d" % i, align_bytes=64) for i in range(len(GROUP))]
+        pair_f32 = [keep.tile([P, 2, K], F32, name="pair_f32_%d" % j) for j in range(CHUNKS)]
+        pair_t = [keep.tile([P, 2 * K], BF16, name="pair_t%d" % j, align_bytes=64) for j in range(CHUNKS)]
+        quad_f32 = dict((j, keep.tile([P, K], F32, name="quad_f32_%d" % j)) for j in (0, 1, 3, 4))
+        quad_t = [keep.tile([P, K], BF16, name="quad_t%d" % j, align_bytes=64) for j in range(CHUNKS)]
+        eight_f32 = [keep.tile([P, K], F32, name="eight_f32_%d" % g) for g in range(2)]
+        ten_t = [keep.tile([P, K], BF16, name="ten_t%d" % g, align_bytes=64) for g in range(2)]
+        w_codes = [keep.tile([P, OUT], U32, name="w_codes%d" % i, align_bytes=64) for i in range(len(GROUP))]
+        w_scales = [keep.tile([P, OUT], U8, name="w_scales%d" % i, align_bytes=64) for i in range(len(GROUP))]
+        widths = (CHUNK * P, 2 * P, P, P)
+        counts = (CHUNKS, CHUNKS, CHUNKS, 2)
+        codes = [
+            [keep.tile([P, widths[i]], U32, name="codes%d_%d" % (i, n), align_bytes=64) for n in range(counts[i])]
+            for i in range(len(GROUP))
+        ]
+        scales = [
+            [keep.tile([P, widths[i]], U8, name="scales%d_%d" % (i, n), align_bytes=64) for n in range(counts[i])]
+            for i in range(len(GROUP))
+        ]
+        quad_row = [keep.tile([P, 1, OUT], F32, name="quad_row%d" % j) for j in range(CHUNKS)]
+        ten_row = [keep.tile([P, 1, OUT], F32, name="ten_row%d" % g) for g in range(2)]
+        ten_rows = keep.tile([P, 5, OUT], F32, name="ten_rows")
+        products = {}
+        out_tiles = {}
+
+        def load_x(j, first, last):
+            nc.sync.dma_start(
+                out=x_in[j][:, first * K : last * K], in_=x_rows[:, (j * CHUNK + first) * K : (j * CHUNK + last) * K]
+            )
+
+        def load_w(i):
+            w_tile = w_pool.tile([P, 4 * K], BF16, name="w_tile", tag="w_tile")
+            w_in[i] = w_tile
+            nc.sync.dma_start(out=w_tile[:], in_=w_rows[i])
+
+        def flip(source, half):
+            words = source[:].bitcast(F32)
+            bank = flip_pool.tile([P, PSUM_BANK], F32, name="bank", tag="bank")
+            for m in range(4):
+                col = (4 * half + m) * P
+                nc.tensor.transpose(bank[:, m * P : (m + 1) * P], words[:, col : col + P], identity[:])
+            return bank
+
+        def flip_x(j, half):
+            bank = flip(x_in[j], half)
+            nc.scalar.copy(
+                out=x_t[j][:].bitcast(F32).rearrange("q (t p u) -> q t p u", t=CHUNK, u=2)[
+                    :, 2 * half : 2 * half + 2, :, :
+                ],
+                in_=bank[:].rearrange("q (t u p) -> q t p u", t=2, u=2),
+            )
+
+        def unpack_w(i, half, bank):
+            nc.scalar.copy(
+                out=w_t[i][:].bitcast(F32).rearrange("q (p h m) -> q p h m", h=2, m=4)[:, :, half, :],
+                in_=bank[:].rearrange("q (m p) -> q p m", m=4),
+            )
+
+        def flip_w(i, half):
+            unpack_w(i, half, flip(w_in[i], half))
+
+        def spread_bias(i):
+            spread = product_pool.tile([P, OUT], F32, name="spread", tag="product")
+            nc.tensor.matmul(out=spread[:], lhsT=ones[:], rhs=bias_in[:, i * OUT : (i + 1) * OUT], start=True, stop=True)
+            nc.scalar.copy(out=bias[:, i, :], in_=spread[:])
 
         def add(dst, a, b):
-            nc.vector.tensor_tensor(out=dst, in0=a, in1=b, op=ALU.add)
+            nc.vector.tensor_tensor(out=dst, in0=a, in1=b, op=ADD)
 
-        def gcopy(dst, src):
-            nc.gpsimd.tensor_scalar(out=dst, in0=src, scalar1=1.0, scalar2=0.0, op0=ALU.mult, op1=ALU.add)
+        def pool_copy(dst, src):
+            nc.gpsimd.tensor_scalar(out=dst, in0=src, scalar1=1.0, scalar2=0.0, op0=MULT, op1=ADD)
 
-        def quant(codes, plane, src):
-            nc.vector.quantize_mx(out=codes.bitcast(FP8X4), scales=plane, in_=src)
+        def sum_pairs(j):
+            tiles = x_t[j][:].rearrange("q (g two n) -> q g two n", g=2, two=2)
+            add(pair_f32[j][:], tiles[:, :, 0, :], tiles[:, :, 1, :])
 
-        def operand(t):
-            n = int(t[1])
-            col = "abcd".index(t[2]) if len(t) > 2 else 0
-            if t[0] == "1":
-                return xc[n], xs[n], col
-            if t[0] == "2":
-                return c2[n], p2[n], col
-            if t[0] == "4":
-                return c4[n], p4[n], 0
-            return cz[n], pz[n], 0
+        def sum_quad(j, dst):
+            add(dst[:], pair_f32[j][:, 0, :], pair_f32[j][:, 1, :])
 
-        def dest(t):
-            n = int(t[1])
-            if t[0] == "4":
-                return row4[n][:, 0, :]
-            if t[0] == "z":
-                return rowz[n][:, 0, :]
-            u = t[0:2]
-            if u not in obs:
-                ob = outp.tile([P, CH, DO], F32, name="ob", tag="ob")
-                obs[u] = ob
-            col = "abcd".index(t[2])
-            if t[0] == "2":
-                return obs[u][:, 2 * col, :]
-            return obs[u][:, col, :]
+        def quantise(i, n, source):
+            nc.vector.quantize_mx(out=codes[i][n][:].bitcast(FP8X4), scales=scales[i][n][:], in_=source[:])
 
-        def relu(rows, r):
-            nc.scalar.activation(out=rows, in_=rows, func=ACT.Relu, scale=1.0 / r)
+        def quantise_w(i):
+            nc.vector.quantize_mx(out=w_codes[i][:].bitcast(FP8X4), scales=w_scales[i][:], in_=w_t[i][:])
 
-        def emit(op):
-            k = op[0]
-            a = op[1:]
-            if op == "mz":
-                nc.vector.memset(bz[:], 0.0)
-                nc.vector.memset(ones[:], 1.0)
-            elif op == "id":
-                make_identity(nc, ident[:])
-            elif op == "Lb":
-                nc.sync.dma_start(out=bz[0:1, :], in_=b_row)
-            elif op[0:2] == "Lx":
-                j = int(op[2])
-                lo = 0
-                hi = CH * D
-                if len(op) > 3:
-                    lo = "ab".index(op[3]) * 2 * D
-                    hi = lo + 2 * D
-                nc.sync.dma_start(out=x_sb[j][:, lo:hi], in_=x_rows[:, j * CH * D + lo : j * CH * D + hi])
-            elif op[0:2] == "LW":
-                i = int(op[2])
-                w_in = wpool.tile([P, 4 * D], BF16, name="w_in", tag="w_in")
-                w_sb[i] = w_in
-                nc.sync.dma_start(out=w_in[:], in_=w_rows[i])
-            elif k == "T":
-                src = (x_sb if a[0] == "x" else w_sb)[int(a[1])][:].bitcast(F32)
-                h = "ab".index(a[2])
-                pt = pst.tile([P, 512], F32, name="pt", tag="pt")
-                banks[a] = pt
-                for m in range(4):
-                    nc.tensor.transpose(pt[:, m * P : (m + 1) * P], src[:, (4 * h + m) * P : (4 * h + m + 1) * P], ident[:])
-            elif op[0:2] == "CB":
-                i = int(op[2])
-                nc.scalar.copy(out=bias[:, i, :], in_=ys["b" + op[2]][:])
-            elif k == "C":
-                n = int(a[1])
-                h = "ab".index(a[2])
-                pt = banks[a]
-                if a[0] == "x":
-                    dst = xg[n][:].bitcast(F32).rearrange("q (t p u) -> q t p u", t=CH, u=2)[:, 2 * h : 2 * h + 2, :, :]
-                    src = pt[:].rearrange("q (t u p) -> q t p u", t=2, u=2)
-                else:
-                    dst = wg[n][:].bitcast(F32).rearrange("q (p h m) -> q p h m", h=2, m=4)[:, :, h, :]
-                    src = pt[:].rearrange("q (m p) -> q p m", m=4)
-                if a in VCOPY:
-                    nc.vector.tensor_copy(out=dst, in_=src)
-                else:
-                    nc.scalar.copy(out=dst, in_=src)
-            elif op[0:2] == "PB":
-                i = int(op[2])
-                pb = psy.tile([P, DO], F32, name="pb", tag="y")
-                ys["b" + op[2]] = pb
-                nc.tensor.matmul(out=pb[:], lhsT=ones[:], rhs=bz[:, i * DO : (i + 1) * DO], start=True, stop=True)
-            elif op[0:2] == "QW":
-                i = int(op[2])
-                quant(wc[i][:], ws[i][:], wg[i][:])
-            elif op[0:2] == "Qx":
-                j = int(op[2])
-                quant(xc[j][:], xs[j][:], xg[j][:])
-            elif op[0:2] == "Q2":
-                j = int(op[2])
-                quant(c2[j][:], p2[j][:], s2b[j][:])
-            elif op[0:2] == "Q4":
-                j = int(op[2])
-                quant(c4[j][:], p4[j][:], s4b[j][:])
-            elif op[0:2] == "Qz":
-                g = int(op[2])
-                quant(cz[g][:], pz[g][:], szb[g][:])
-            elif k == "A":
-                j = int(a)
-                xg4 = xg[j][:].rearrange("q (g j n) -> q g j n", g=2, j=2)
-                add(s2f[j][:], xg4[:, :, 0, :], xg4[:, :, 1, :])
-            elif k == "B":
-                j = int(a)
-                add(s4f[j][:], s2f[j][:, 0, :], s2f[j][:, 1, :])
-            elif k == "H":
-                j = int(a)
-                add(s4b[j][:], s2f[j][:, 0, :], s2f[j][:, 1, :])
-            elif op == "acc0":
-                add(acc[0][:], s4f[0][:], s4f[1][:])
-            elif op == "sz0":
-                add(szb[0][:], acc[0][:], s2f[2][:, 0, :])
-            elif op == "acc1":
-                add(acc[1][:], s2f[2][:, 1, :], s4f[3][:])
-            elif op == "sz1":
-                add(szb[1][:], acc[1][:], s4f[4][:])
-            elif op[0:2] == "K4":
-                j = int(op[2])
-                gcopy(s4b[j][:], s4f[j][:])
-            elif op[0:2] == "K2":
-                j = int(op[2])
-                gcopy(s2b[j][:], s2f[j][:].rearrange("q g n -> q (g n)"))
-            elif k == "M":
-                codes, plane, col = operand(a)
-                i = WIDX[a[0]]
-                y = psy.tile([P, DO], F32, name="y", tag="y")
-                ys[a] = y
-                nc.tensor.matmul_mx(
-                    out=y[:],
-                    lhsT=codes[:, col * P : (col + 1) * P].bitcast(FP8X4),
-                    lhsT_scale=plane[:, col * P : (col + 1) * P],
-                    rhs=wc[i][:].bitcast(FP8X4),
-                    rhs_scale=ws[i][:],
-                    start=True,
-                    stop=True,
-                )
-            elif k == "E":
-                add(dest(a), ys[a][:], bias[:, WIDX[a[0]], :])
-            elif k == "R":
-                n = int(a[1])
-                if a[0] == "4" and a in FULL:
-                    ob = outp.tile([P, CH, DO], F32, name="ob", tag="ob")
-                    obs[a] = ob
-                    nc.scalar.activation(out=ob[:], in_=row4[n][:].to_broadcast([P, CH, DO]), func=ACT.Relu, scale=0.25)
-                elif a[0] == "z" and a in FULL:
-                    nc.scalar.activation(out=obz[:], in_=rowz[n][:].to_broadcast([P, 5, DO]), func=ACT.Relu, scale=0.1)
-                elif a[0] == "4":
-                    relu(row4[n][:], 4)
-                elif a[0] == "z":
-                    relu(rowz[n][:], 10)
-                elif a[0] == "2":
-                    relu(obs[a[0:2]][:].rearrange("p (g j) d -> p g j d", j=2)[:, :, 0, :], 2)
-                else:
-                    h = "ab".index(a[2])
-                    relu(obs[a[0:2]][:, 2 * h : 2 * h + 2, :], 1)
-            elif op[0:2] == "X2":
-                ob4 = obs[a][:].rearrange("p (g j) d -> p g j d", j=2)
-                gcopy(ob4[:, :, 1, :], ob4[:, :, 0, :])
-            elif k == "S":
-                n = int(a[1])
-                if a[0] == "z" and a in FULL:
-                    for h in range(2):
-                        row = 10 * n + 5 * h
-                        nc.sync.dma_start(out=out_rows[3, :, row : row + 5, :], in_=obz[:])
-                elif a[0] == "4" and a not in FULL:
-                    nc.sync.dma_start(out=out_rows[2, :, n * CH : (n + 1) * CH, :], in_=row4[n][:].to_broadcast([P, CH, DO]))
-                elif a[0] == "z":
-                    row = 10 * n
-                    for cnt in (4, 4, 2):
-                        nc.sync.dma_start(out=out_rows[3, :, row : row + cnt, :], in_=rowz[n][:].to_broadcast([P, cnt, DO]))
-                        row += cnt
-                else:
-                    nc.sync.dma_start(out=out_rows[WIDX[a[0]], :, n * CH : (n + 1) * CH, :], in_=obs[a][:])
-            else:
-                raise ValueError(op)
+        def multiply(i, n):
+            per_tile = widths[i] // P
+            cols = slice((n % per_tile) * P, (n % per_tile + 1) * P)
+            product = product_pool.tile([P, OUT], F32, name="product", tag="product")
+            products[(i, n)] = product
+            nc.tensor.matmul_mx(
+                out=product[:],
+                lhsT=codes[i][n // per_tile][:, cols].bitcast(FP8X4),
+                lhsT_scale=scales[i][n // per_tile][:, cols],
+                rhs=w_codes[i][:].bitcast(FP8X4),
+                rhs_scale=w_scales[i][:],
+                start=True,
+                stop=True,
+            )
 
-        for op in ORDER:
-            emit(op)
+        def add_bias(i, n, dst):
+            add(dst, products[(i, n)][:], bias[:, i, :])
+
+        def relu(i, dst, src):
+            nc.scalar.activation(out=dst, in_=src, func=RELU, scale=1.0 / GROUP[i])
+
+        def store(i, first, src):
+            nc.sync.dma_start(out=out_rows[i, :, first : first + src.shape[1], :], in_=src)
+
+        def finish_row(i, first, row, cuts):
+            relu(i, row[:], row[:])
+            for count in cuts:
+                store(i, first, row[:].to_broadcast([P, count, OUT]))
+                first += count
+
+        def finish_quad(j):
+            rows = out_pool.tile([P, CHUNK, OUT], F32, name="rows", tag="rows")
+            relu(2, rows[:], quad_row[j][:].to_broadcast([P, CHUNK, OUT]))
+            store(2, j * CHUNK, rows[:])
+
+        nc.vector.memset(bias_in[:], 0.0)
+        nc.vector.memset(ones[:], 1.0)
+        make_identity(nc, identity[:])
+        load_x(0, 0, 2)
+        load_x(0, 2, 4)
+        load_w(2)
+        load_x(1, 0, CHUNK)
+        load_x(2, 0, CHUNK)
+        nc.sync.dma_start(out=bias_in[0:1, :], in_=bias_row)
+        load_w(3)
+        load_x(3, 0, CHUNK)
+        load_x(4, 0, CHUNK)
+
+        flip_x(0, 0)
+        flip_x(0, 1)
+        flip_w(2, 0)
+        flip_w(2, 1)
+        load_w(1)
+        sum_pairs(0)
+        sum_quad(0, quad_t[0])
+        quantise(2, 0, quad_t[0])
+        sum_quad(0, quad_f32[0])
+        quantise_w(2)
+        flip_x(1, 0)
+        flip_x(1, 1)
+        spread_bias(2)
+        flip_x(2, 0)
+        flip_x(2, 1)
+        multiply(2, 0)
+        sum_pairs(1)
+        sum_quad(1, quad_f32[1])
+        pool_copy(quad_t[1][:], quad_f32[1][:])
+        add_bias(2, 0, quad_row[0][:, 0, :])
+        flip_w(3, 0)
+        spread_bias(3)
+        last_bank = flip(w_in[3], 1)
+        load_w(0)
+        finish_row(2, 0, quad_row[0], (CHUNK,))
+        unpack_w(3, 1, last_bank)
+        add(eight_f32[0][:], quad_f32[0][:], quad_f32[1][:])
+        quantise(2, 1, quad_t[1])
+        flip_x(3, 0)
+        multiply(2, 1)
+        flip_x(3, 1)
+        sum_pairs(2)
+        add_bias(2, 1, quad_row[1][:, 0, :])
+        finish_row(2, CHUNK, quad_row[1], (CHUNK,))
+        quantise_w(3)
+        add(ten_t[0][:], eight_f32[0][:], pair_f32[2][:, 0, :])
+        quantise(3, 0, ten_t[0])
+        sum_quad(2, quad_t[2])
+        quantise(2, 2, quad_t[2])
+        flip_x(4, 0)
+        flip_x(4, 1)
+        multiply(3, 0)
+        add_bias(3, 0, ten_row[0][:, 0, :])
+        finish_row(3, 0, ten_row[0], (4, 4, 2))
+        flip_w(1, 0)
+        multiply(2, 2)
+        flip_w(1, 1)
+        flip_w(0, 0)
+        sum_pairs(3)
+        sum_quad(3, quad_f32[3])
+        pool_copy(quad_t[3][:], quad_f32[3][:])
+        add_bias(2, 2, quad_row[2][:, 0, :])
+        finish_quad(2)
+        sum_pairs(4)
+        quantise(2, 3, quad_t[3])
+        multiply(2, 3)
+        sum_quad(4, quad_f32[4])
+        pool_copy(quad_t[4][:], quad_f32[4][:])
+        add(eight_f32[1][:], pair_f32[2][:, 1, :], quad_f32[3][:])
+        add_bias(2, 3, quad_row[3][:, 0, :])
+        finish_quad(3)
+        add(ten_t[1][:], eight_f32[1][:], quad_f32[4][:])
+        quantise(3, 1, ten_t[1])
+        multiply(3, 1)
+        add_bias(3, 1, ten_row[1][:, 0, :])
+        relu(3, ten_rows[:], ten_row[1][:].to_broadcast([P, 5, OUT]))
+        store(3, 10, ten_rows[:])
+        store(3, 15, ten_rows[:])
+        flip_w(0, 1)
+        quantise(2, 4, quad_t[4])
+        multiply(2, 4)
+        spread_bias(1)
+        spread_bias(0)
+        for j in range(CHUNKS):
+            pool_copy(pair_t[j][:], pair_f32[j][:].rearrange("q g n -> q (g n)"))
+        quantise_w(1)
+        quantise(0, 0, x_t[0])
+        quantise(1, 0, pair_t[0])
+        add_bias(2, 4, quad_row[4][:, 0, :])
+        quantise_w(0)
+        finish_quad(4)
+
+        passes = []
+        for j in range(CHUNKS):
+            passes.extend((1, 2 * j + g) for g in range(2))
+            passes.extend((0, CHUNK * j + t) for t in range(CHUNK))
+        for i, n in passes[:PRODUCT_BANKS]:
+            multiply(i, n)
+        for step, (i, n) in enumerate(passes):
+            per_chunk = CHUNK // GROUP[i]
+            j = n // per_chunk
+            place = n % per_chunk
+            if place == 0:
+                rows = out_pool.tile([P, CHUNK, OUT], F32, name="rows", tag="rows")
+                out_tiles[i] = rows
+            rows = out_tiles[i]
+            add_bias(i, n, rows[:, place * GROUP[i], :])
+            if place == 1 and j + 1 < CHUNKS:
+                quantise(i, j + 1, (x_t, pair_t)[i][j + 1])
+            if step + PRODUCT_BANKS < len(passes):
+                multiply(*passes[step + PRODUCT_BANKS])
+            if i == 1 and place == 1:
+                twice = rows[:].rearrange("p (g two) d -> p g two d", two=2)
+                relu(1, twice[:, :, 0, :], twice[:, :, 0, :])
+                pool_copy(twice[:, :, 1, :], twice[:, :, 0, :])
+                store(1, j * CHUNK, rows[:])
+            if i == 0 and place % 2 == 1:
+                relu(0, rows[:, place - 1 : place + 1, :], rows[:, place - 1 : place + 1, :])
+            if i == 0 and place == CHUNK - 1:
+                store(0, j * CHUNK, rows[:])

from contextlib import ExitStack

import concourse.mybir as mybir
from concourse.masks import make_identity

F32 = mybir.dt.float32
BF16 = mybir.dt.bfloat16
U32 = mybir.dt.uint32
U8 = mybir.dt.uint8
FP8X4 = mybir.dt.float8_e4m3fn_x4
ADD = mybir.AluOpType.add
MULT = mybir.AluOpType.mult
RELU = mybir.ActivationFunctionType.Relu

P = 128
ROWS = 2560
K = 512
OUT = 512
GROUP = (1, 2, 4, 10)
TILES = ROWS // P
CHUNK = 4
CHUNKS = TILES // CHUNK
PSUM_BANK = 512
PRODUCT_BANKS = 5
FLOPS = 2 * sum(ROWS // r for r in GROUP) * K * OUT


def tile_contractexpand_pa_kernel(tc, inputs_c_e, Ws, bs, out):
    nc = tc.nc
    x_rows = inputs_c_e.rearrange("(p t) k -> p (t k)", t=TILES)
    w_rows = Ws.rearrange("i (p c) k -> i p (c k)", c=4)
    bias_row = bs.rearrange("(o i) d -> o (i d)", o=1)
    out_rows = out.rearrange("(i p t) d -> i p t d", i=len(GROUP), t=TILES)

    with ExitStack() as ctx:
        keep = ctx.enter_context(tc.tile_pool(name="keep", bufs=1))
        w_pool = ctx.enter_context(tc.tile_pool(name="w_pool", bufs=2))
        out_pool = ctx.enter_context(tc.tile_pool(name="out_pool", bufs=6))
        flip_pool = ctx.enter_context(tc.psum_pool(name="flip_pool", bufs=8 - PRODUCT_BANKS))
        product_pool = ctx.enter_context(tc.psum_pool(name="product_pool", bufs=PRODUCT_BANKS))
        ctx.enter_context(tc.manual_schedule())

        identity = keep.tile([P, P], F32, name="identity")
        ones = keep.tile([P, P], BF16, name="ones")
        bias_in = keep.tile([P, len(GROUP) * OUT], BF16, name="bias_in")
        bias = keep.tile([P, len(GROUP), OUT], F32, name="bias")
        x_in = [keep.tile([P, CHUNK * K], BF16, name="x_in%d" % j) for j in range(CHUNKS)]
        w_in = {}
        x_t = [keep.tile([P, CHUNK * K], BF16, name="x_t%d" % j, align_bytes=64) for j in range(CHUNKS)]
        w_t = [keep.tile([P, 4 * OUT], BF16, name="w_t%d" % i, align_bytes=64) for i in range(len(GROUP))]
        pair_f32 = [keep.tile([P, 2, K], F32, name="pair_f32_%d" % j) for j in range(CHUNKS)]
        pair_t = [keep.tile([P, 2 * K], BF16, name="pair_t%d" % j, align_bytes=64) for j in range(CHUNKS)]
        quad_f32 = dict((j, keep.tile([P, K], F32, name="quad_f32_%d" % j)) for j in (0, 1, 3, 4))
        quad_t = [keep.tile([P, K], BF16, name="quad_t%d" % j, align_bytes=64) for j in range(CHUNKS)]
        eight_f32 = [keep.tile([P, K], F32, name="eight_f32_%d" % g) for g in range(2)]
        ten_t = [keep.tile([P, K], BF16, name="ten_t%d" % g, align_bytes=64) for g in range(2)]
        w_codes = [keep.tile([P, OUT], U32, name="w_codes%d" % i, align_bytes=64) for i in range(len(GROUP))]
        w_scales = [keep.tile([P, OUT], U8, name="w_scales%d" % i, align_bytes=64) for i in range(len(GROUP))]
        widths = (CHUNK * P, 2 * P, P, P)
        counts = (CHUNKS, CHUNKS, CHUNKS, 2)
        codes = [
            [keep.tile([P, widths[i]], U32, name="codes%d_%d" % (i, n), align_bytes=64) for n in range(counts[i])]
            for i in range(len(GROUP))
        ]
        scales = [
            [keep.tile([P, widths[i]], U8, name="scales%d_%d" % (i, n), align_bytes=64) for n in range(counts[i])]
            for i in range(len(GROUP))
        ]
        quad_row = [keep.tile([P, 1, OUT], F32, name="quad_row%d" % j) for j in range(CHUNKS)]
        ten_row = [keep.tile([P, 1, OUT], F32, name="ten_row%d" % g) for g in range(2)]
        ten_rows = keep.tile([P, 5, OUT], F32, name="ten_rows")
        products = {}
        out_tiles = {}

        def load_x(j, first, last):
            nc.sync.dma_start(
                out=x_in[j][:, first * K : last * K], in_=x_rows[:, (j * CHUNK + first) * K : (j * CHUNK + last) * K]
            )

        def load_w(i):
            w_tile = w_pool.tile([P, 4 * K], BF16, name="w_tile", tag="w_tile")
            w_in[i] = w_tile
            nc.sync.dma_start(out=w_tile[:], in_=w_rows[i])

        def flip(source, half):
            words = source[:].bitcast(F32)
            bank = flip_pool.tile([P, PSUM_BANK], F32, name="bank", tag="bank")
            for m in range(4):
                col = (4 * half + m) * P
                nc.tensor.transpose(bank[:, m * P : (m + 1) * P], words[:, col : col + P], identity[:])
            return bank

        def flip_x(j, half):
            bank = flip(x_in[j], half)
            nc.scalar.copy(
                out=x_t[j][:].bitcast(F32).rearrange("q (t p u) -> q t p u", t=CHUNK, u=2)[
                    :, 2 * half : 2 * half + 2, :, :
                ],
                in_=bank[:].rearrange("q (t u p) -> q t p u", t=2, u=2),
            )

        def unpack_w(i, half, bank):
            nc.scalar.copy(
                out=w_t[i][:].bitcast(F32).rearrange("q (p h m) -> q p h m", h=2, m=4)[:, :, half, :],
                in_=bank[:].rearrange("q (m p) -> q p m", m=4),
            )

        def flip_w(i, half):
            unpack_w(i, half, flip(w_in[i], half))

        def spread_bias(i):
            spread = product_pool.tile([P, OUT], F32, name="spread", tag="product")
            nc.tensor.matmul(out=spread[:], lhsT=ones[:], rhs=bias_in[:, i * OUT : (i + 1) * OUT], start=True, stop=True)
            nc.scalar.copy(out=bias[:, i, :], in_=spread[:])

        def add(dst, a, b):
            nc.vector.tensor_tensor(out=dst, in0=a, in1=b, op=ADD)

        def pool_copy(dst, src):
            nc.gpsimd.tensor_scalar(out=dst, in0=src, scalar1=1.0, scalar2=0.0, op0=MULT, op1=ADD)

        def sum_pairs(j):
            tiles = x_t[j][:].rearrange("q (g two n) -> q g two n", g=2, two=2)
            add(pair_f32[j][:], tiles[:, :, 0, :], tiles[:, :, 1, :])

        def sum_quad(j, dst):
            add(dst[:], pair_f32[j][:, 0, :], pair_f32[j][:, 1, :])

        def quantise(i, n, source):
            nc.vector.quantize_mx(out=codes[i][n][:].bitcast(FP8X4), scales=scales[i][n][:], in_=source[:])

        def quantise_w(i):
            nc.vector.quantize_mx(out=w_codes[i][:].bitcast(FP8X4), scales=w_scales[i][:], in_=w_t[i][:])

        def multiply(i, n):
            per_tile = widths[i] // P
            cols = slice((n % per_tile) * P, (n % per_tile + 1) * P)
            product = product_pool.tile([P, OUT], F32, name="product", tag="product")
            products[(i, n)] = product
            nc.tensor.matmul_mx(
                out=product[:],
                lhsT=codes[i][n // per_tile][:, cols].bitcast(FP8X4),
                lhsT_scale=scales[i][n // per_tile][:, cols],
                rhs=w_codes[i][:].bitcast(FP8X4),
                rhs_scale=w_scales[i][:],
                start=True,
                stop=True,
            )

        def add_bias(i, n, dst):
            add(dst, products[(i, n)][:], bias[:, i, :])

        def relu(i, dst, src):
            nc.scalar.activation(out=dst, in_=src, func=RELU, scale=1.0 / GROUP[i])

        def store(i, first, src):
            nc.sync.dma_start(out=out_rows[i, :, first : first + src.shape[1], :], in_=src)

        def finish_row(i, first, row, cuts):
            relu(i, row[:], row[:])
            for count in cuts:
                store(i, first, row[:].to_broadcast([P, count, OUT]))
                first += count

        def finish_quad(j):
            rows = out_pool.tile([P, CHUNK, OUT], F32, name="rows", tag="rows")
            relu(2, rows[:], quad_row[j][:].to_broadcast([P, CHUNK, OUT]))
            store(2, j * CHUNK, rows[:])

        nc.vector.memset(bias_in[:], 0.0)
        nc.vector.memset(ones[:], 1.0)
        make_identity(nc, identity[:])
        load_x(0, 0, 2)
        load_x(0, 2, 4)
        load_w(2)
        load_x(1, 0, CHUNK)
        load_x(2, 0, CHUNK)
        nc.sync.dma_start(out=bias_in[0:1, :], in_=bias_row)
        load_w(3)
        load_x(3, 0, CHUNK)
        load_x(4, 0, CHUNK)

        flip_x(0, 0)
        flip_x(0, 1)
        flip_w(2, 0)
        flip_w(2, 1)
        load_w(1)
        sum_pairs(0)
        sum_quad(0, quad_t[0])
        quantise(2, 0, quad_t[0])
        sum_quad(0, quad_f32[0])
        quantise_w(2)
        flip_x(1, 0)
        flip_x(1, 1)
        spread_bias(2)
        flip_x(2, 0)
        flip_x(2, 1)
        multiply(2, 0)
        sum_pairs(1)
        sum_quad(1, quad_f32[1])
        pool_copy(quad_t[1][:], quad_f32[1][:])
        add_bias(2, 0, quad_row[0][:, 0, :])
        flip_w(3, 0)
        spread_bias(3)
        last_bank = flip(w_in[3], 1)
        load_w(0)
        finish_row(2, 0, quad_row[0], (CHUNK,))
        unpack_w(3, 1, last_bank)
        add(eight_f32[0][:], quad_f32[0][:], quad_f32[1][:])
        quantise(2, 1, quad_t[1])
        flip_x(3, 0)
        multiply(2, 1)
        flip_x(3, 1)
        sum_pairs(2)
        add_bias(2, 1, quad_row[1][:, 0, :])
        finish_row(2, CHUNK, quad_row[1], (CHUNK,))
        quantise_w(3)
        add(ten_t[0][:], eight_f32[0][:], pair_f32[2][:, 0, :])
        quantise(3, 0, ten_t[0])
        sum_quad(2, quad_t[2])
        quantise(2, 2, quad_t[2])
        flip_x(4, 0)
        flip_x(4, 1)
        multiply(3, 0)
        add_bias(3, 0, ten_row[0][:, 0, :])
        finish_row(3, 0, ten_row[0], (4, 4, 2))
        flip_w(1, 0)
        multiply(2, 2)
        flip_w(1, 1)
        flip_w(0, 0)
        sum_pairs(3)
        sum_quad(3, quad_f32[3])
        pool_copy(quad_t[3][:], quad_f32[3][:])
        add_bias(2, 2, quad_row[2][:, 0, :])
        finish_quad(2)
        sum_pairs(4)
        quantise(2, 3, quad_t[3])
        multiply(2, 3)
        sum_quad(4, quad_f32[4])
        pool_copy(quad_t[4][:], quad_f32[4][:])
        add(eight_f32[1][:], pair_f32[2][:, 1, :], quad_f32[3][:])
        add_bias(2, 3, quad_row[3][:, 0, :])
        finish_quad(3)
        add(ten_t[1][:], eight_f32[1][:], quad_f32[4][:])
        quantise(3, 1, ten_t[1])
        multiply(3, 1)
        add_bias(3, 1, ten_row[1][:, 0, :])
        relu(3, ten_rows[:], ten_row[1][:].to_broadcast([P, 5, OUT]))
        store(3, 10, ten_rows[:])
        store(3, 15, ten_rows[:])
        flip_w(0, 1)
        quantise(2, 4, quad_t[4])
        multiply(2, 4)
        spread_bias(1)
        spread_bias(0)
        for j in range(CHUNKS):
            pool_copy(pair_t[j][:], pair_f32[j][:].rearrange("q g n -> q (g n)"))
        quantise_w(1)
        quantise(0, 0, x_t[0])
        quantise(1, 0, pair_t[0])
        add_bias(2, 4, quad_row[4][:, 0, :])
        quantise_w(0)
        finish_quad(4)

        passes = []
        for j in range(CHUNKS):
            passes.extend((1, 2 * j + g) for g in range(2))
            passes.extend((0, CHUNK * j + t) for t in range(CHUNK))
        for i, n in passes[:PRODUCT_BANKS]:
            multiply(i, n)
        for step, (i, n) in enumerate(passes):
            per_chunk = CHUNK // GROUP[i]
            j = n // per_chunk
            place = n % per_chunk
            if place == 0:
                rows = out_pool.tile([P, CHUNK, OUT], F32, name="rows", tag="rows")
                out_tiles[i] = rows
            rows = out_tiles[i]
            add_bias(i, n, rows[:, place * GROUP[i], :])
            if place == 1 and j + 1 < CHUNKS:
                quantise(i, j + 1, (x_t, pair_t)[i][j + 1])
            if step + PRODUCT_BANKS < len(passes):
                multiply(*passes[step + PRODUCT_BANKS])
            if i == 1 and place == 1:
                twice = rows[:].rearrange("p (g two) d -> p g two d", two=2)
                relu(1, twice[:, :, 0, :], twice[:, :, 0, :])
                pool_copy(twice[:, :, 1, :], twice[:, :, 0, :])
                store(1, j * CHUNK, rows[:])
            if i == 0 and place % 2 == 1:
                relu(0, rows[:, place - 1 : place + 1, :], rows[:, place - 1 : place + 1, :])
            if i == 0 and place == CHUNK - 1:
                store(0, j * CHUNK, rows[:])
